import numpy as np
import ml_dtypes


def mxq(x, axis, fmt="e4m3"):
    dtype, down = {"e4m3": (ml_dtypes.float8_e4m3fn, 7), "e5m2": (ml_dtypes.float8_e5m2, 14)}[fmt]
    v = np.moveaxis(np.asarray(x, np.float32).astype(ml_dtypes.bfloat16).astype(np.float64), axis, -1)
    blocks = v.reshape(v.shape[:-1] + (-1, 32))
    amax = np.abs(blocks).max(-1, keepdims=True)
    byte = np.maximum(np.where(amax > 0, np.frexp(amax)[1] - 1 + 127, 0) - down, 1)
    scale = np.exp2(byte - 127.0)
    codes = (blocks / scale).astype(np.float32).astype(dtype).astype(np.float64)
    return np.moveaxis((codes * scale).reshape(v.shape), -1, axis)


WIDE = False


def mx_kscale(k):
    if not WIDE:
        return np.ones(k)
    levels = np.array([10, -10, 5, -5, 0])
    if k % 512:
        return np.exp2(np.random.permutation(np.resize(levels, k // 32))).repeat(32)
    a = np.empty((k // 512, 16))
    for p in range(k // 512):
        a[p, :8] = np.random.permutation(np.resize(levels, 8))
        for g in range(8):
            far = levels[np.abs(levels - a[p, g]) >= 10]
            a[p, g + 8] = far[np.random.randint(len(far))]
    return np.exp2(a.ravel()).repeat(32)


BF16 = ml_dtypes.bfloat16


def bf(x):
    return np.asarray(x, np.float32).astype(BF16)


def f64(x):
    return np.asarray(x).astype(np.float64)


B, N, F, DIM, H, DH, D3 = 2, 24, 16, 1024, 12, 64, 512
W = H * D3
SCALE = 1.0 / (np.sqrt(DH) * H)
QS = np.sqrt(1.5 / (SCALE * np.sqrt(D3)))


def setup_inputs():
    s, t = mx_kscale(DIM), mx_kscale(D3)
    th = np.tile(t, H)
    return {"x": bf(np.random.standard_normal((B, N * F, DIM)) * s),
            "Wq": bf(np.random.standard_normal((DIM, W)) * QS / np.sqrt(DIM) / s[:, None] * th),
            "bq": bf(np.random.standard_normal(W) * 0.2 * QS * th),
            "k": bf(np.random.standard_normal((B, H, N, F, D3)) * QS / t)}


def reference(x, Wq, bq, k):
    y = (mxq(f64(x), 2, "e4m3") @ mxq(f64(Wq), 0, "e4m3")) + f64(bq)
    q = y.reshape(B, F, N, H, D3).transpose(0, 3, 2, 1, 4)
    s = (mxq(q, 4, "e4m3") @ mxq(f64(k), 4, "e4m3").transpose(0, 1, 2, 4, 3)) * SCALE
    e = np.exp(s - s.max(-1, keepdims=True))
    return e / e.sum(-1, keepdims=True)

@@ -1,0 +1,433 @@
+from contextlib import ExitStack
+
+import concourse.mybir as mybir
+from concourse.masks import make_identity
+
+F32 = mybir.dt.float32
+BF16 = mybir.dt.bfloat16
+U32 = mybir.dt.uint32
+U8 = mybir.dt.uint8
+FP8X4 = mybir.dt.float8_e4m3fn_x4
+ALU = mybir.AluOpType
+ACT = mybir.ActivationFunctionType
+AX = mybir.AxisListType
+
+P = 128
+HEADS = 12
+LAST = HEADS - 1
+FLOPS = 2 * 768 * 1024 * 6144 + 2 * 576 * 16 * 16 * 512
+SCALE = 1.0 / 96.0
+BIG = 2.0 ** 100
+BATCHES = ((0, 4), (4, 8), (8, 11), (11, 12))
+REGROUP_ENGINES = {0: "vsvs", 1: "sssg", 2: "sgsg"}
+REGROUP_DEFAULT = "sssg"
+SG_FIRST = ()
+SG_TILES = (0, 1)
+SG_LAST = (0, 1)
+STEADY_STEPS = (
+    ("qw", 1),
+    ("mm", 0, 0),
+    ("mm", 0, 1),
+    ("e", 0, 0),
+    ("mm", 0, 2),
+    ("e", 0, 1),
+    ("mm", 0, 5),
+    ("rg", 2),
+    ("e", 0, 2),
+    ("lw", 4),
+    ("sm", 4),
+    ("mm", 0, 4),
+    ("s2", -1),
+    ("mm", 0, 3),
+    ("ex", -1, 0),
+    ("sm", 1),
+    ("sm", 5),
+    ("e", 0, 4),
+    ("sm", 3),
+    ("kt", 0),
+    ("e", 0, 5),
+    ("lk", 2),
+    ("e", 0, 3),
+    ("ex", -1, 1),
+    ("qqb", 0),
+    ("sm", 2),
+    ("qqa", 0),
+    ("ke", 0),
+    ("qk", 0),
+)
+FIRST_STEPS = (
+    ("mm", 0, 0),
+    ("e", 0, 0),
+    ("mm", 0, 2),
+    ("mm", 0, 1),
+    ("e", 0, 1),
+    ("mm", 0, 3),
+    ("e", 0, 2),
+    ("lk", 2),
+    ("mm", 0, 5),
+    ("e", 0, 3),
+    ("qw", 1),
+    ("mm", 0, 4),
+    ("e", 0, 5),
+    ("rg", 2),
+    ("kt", 0),
+    ("e", 0, 4),
+    ("ke", 0),
+    ("qqb", 0),
+    ("qqa", 0),
+    ("qk", 0),
+    ("lw", 4),
+)
+LAST_STEPS = (
+    ("sm", 4),
+    ("mm", 0, 1),
+    ("mm", 0, 0),
+    ("mm", 0, 2),
+    ("e", 0, 2),
+    ("e", 0, 0),
+    ("s2", -1),
+    ("ex", -1, 1),
+    ("ex", -1, 0),
+    ("sm", 1),
+    ("e", 0, 1),
+    ("mm", 0, 5),
+    ("sm", 5),
+    ("e", 0, 5),
+    ("mm", 0, 3),
+    ("e", 0, 3),
+    ("sm", 2),
+    ("mm", 0, 4),
+    ("kt", 0),
+    ("e", 0, 4),
+    ("ke", 0),
+    ("qq", 0, 0, 1024),
+    ("qq", 0, 2560, 512),
+    ("qq", 0, 1024, 1024),
+    ("qk", 0),
+    ("s2b", 0, 0),
+    ("sm", 3),
+    ("qq", 0, 2048, 512),
+    ("sm", 4),
+    ("ex", 0, 0),
+    ("sm", 5),
+    ("s2b", 0, 1),
+    ("ex", 0, 1),
+    ("sm", 1),
+    ("sm", 2),
+    ("sm", 3),
+    ("sm", 4),
+    ("sm", 5),
+)
+
+
+def tile_dividedspacetimeattention_pa_kernel(tc, x, Wq, bq, k, out):
+    nc = tc.nc
+    with ExitStack() as ctx:
+        consts = ctx.enter_context(tc.tile_pool(name="consts", bufs=1))
+        wraw_p = ctx.enter_context(tc.tile_pool(name="wraw", bufs=4))
+        kraw_p = ctx.enter_context(tc.tile_pool(name="kraw", bufs=3))
+        wg_p = ctx.enter_context(tc.tile_pool(name="wg", bufs=3))
+        wq_p = ctx.enter_context(tc.tile_pool(name="wq", bufs=2))
+        kg_p = ctx.enter_context(tc.tile_pool(name="kg", bufs=2))
+        kq_p = ctx.enter_context(tc.tile_pool(name="kq", bufs=2))
+        qg_p = ctx.enter_context(tc.tile_pool(name="qg", bufs=2))
+        qq_p = ctx.enter_context(tc.tile_pool(name="qq", bufs=2))
+        yf_p = ctx.enter_context(tc.tile_pool(name="yf", bufs=2))
+        sm_p = ctx.enter_context(tc.tile_pool(name="sm", bufs=2))
+        ps_y = ctx.enter_context(tc.psum_pool(name="psy", bufs=3))
+        ps_t = ctx.enter_context(tc.psum_pool(name="pst", bufs=3))
+        ps_s = ctx.enter_context(tc.psum_pool(name="pss", bufs=2))
+        ctx.enter_context(tc.manual_schedule())
+
+        wraw, kraw, wgs, wcs, kgs, kcs, qgs, qcs, ys, yfs, kts, scs = {}, {}, {}, {}, {}, {}, {}, {}, {}, {}, {}, {}
+        zts, ets, mxss, recs = {}, {}, {}, {}
+
+        def copy_on(eng, dst, src):
+            if eng == "v":
+                nc.vector.tensor_copy(out=dst, in_=src)
+            elif eng == "s":
+                nc.scalar.copy(out=dst, in_=src)
+            else:
+                nc.gpsimd.tensor_scalar(out=dst, in0=src, scalar1=1.0, scalar2=0.0, op0=ALU.mult, op1=ALU.add)
+
+        def quant(src, codes, scales, lo, width):
+            nc.vector.quantize_mx(
+                out=codes[:, lo // 4:(lo + width) // 4].bitcast(FP8X4),
+                scales=scales[:, lo // 4:(lo + width) // 4],
+                in_=src[:, lo:lo + width],
+            )
+
+        def mx(dst, a, a_s, a0, b, b_s, b0, start, stop):
+            nc.tensor.matmul_mx(
+                out=dst,
+                lhsT=a[:, a0:a0 + P].bitcast(FP8X4),
+                lhsT_scale=a_s[:, a0:a0 + P],
+                rhs=b[:, b0:b0 + P].bitcast(FP8X4),
+                rhs_scale=b_s[:, b0:b0 + P],
+                start=start,
+                stop=stop,
+            )
+
+        def load_w(h):
+            w_raw = wraw_p.tile([P, 4096], BF16)
+            wv = w_raw[:].rearrange("p (c j w) -> p c j w", c=2, j=4)
+            for c in range(2):
+                nc.sync.dma_start(
+                    out=wv[:, c],
+                    in_=Wq[512 * c:512 * (c + 1), h * 512:(h + 1) * 512].rearrange("(p j) w -> p j w", j=4),
+                )
+            wraw[h] = w_raw
+
+        k_rows = k.rearrange("b h n g d -> b h (n g) d")
+
+        def load_k(h):
+            k_raw = kraw_p.tile([P, 3072], BF16)
+            kv = k_raw[:].rearrange("p (i d) -> p i d", i=6)
+            for b in range(2):
+                nc.sync.dma_start(
+                    out=kv[:, 3 * b:3 * b + 3, :],
+                    in_=k_rows[b, h].rearrange("(s p) d -> p s d", s=3),
+                )
+            kraw[h] = k_raw
+
+        ident = consts.tile([P, P], F32)
+        make_identity(nc, ident[:])
+        warm = consts.tile([P, 2], F32)
+        nc.vector.memset(warm[:], 0.0)
+        nc.scalar.activation(out=warm[:, 1:2], in_=warm[:, 0:1], func=ACT.Exp)
+        b_raw = consts.tile([P, 512], BF16)
+        nc.vector.memset(b_raw[:], 0.0)
+        mask_in = consts.tile([P, 1024], BF16, align_bytes=64)
+        nc.vector.memset(mask_in[:], 0.0)
+
+        x_raw = consts.tile([P, 6144], BF16)
+        xr_v = x_raw[:].rearrange("p (b r c) -> p b r c", b=2, r=3)
+
+        def load_x(b):
+            nc.sync.dma_start(out=xr_v[:, b], in_=x[b].rearrange("(p r) c -> p r c", r=3))
+
+        load_x(0)
+        nc.sync.dma_start(out=b_raw[0:12, :], in_=bq.rearrange("(r c) -> r c", c=512))
+        load_w(0)
+        load_x(1)
+        load_w(1)
+        load_w(2)
+        load_k(0)
+        load_w(3)
+        load_k(1)
+
+        mv = mask_in[:].rearrange("p (o a f j) -> p o a f j", o=2, a=8, f=16)
+        eye8 = ident[:, 0:8].unsqueeze(2).to_broadcast([P, 8, 16])
+        nc.vector.tensor_copy(out=mv[:, 0, :, :, 0], in_=eye8)
+        nc.vector.tensor_scalar(out=mv[:, 1, :, :, 0], in0=eye8, scalar1=-1.0, scalar2=BIG, op0=ALU.add, op1=ALU.mult)
+        mask_c = consts.tile([P, 256], U32, align_bytes=64)
+        mask_s = consts.tile([P, 256], U8, align_bytes=64)
+        quant(mask_in, mask_c, mask_s, 0, 1024)
+
+        bt = ps_t.tile([P, 512], F32, tag="t")
+        b_words = b_raw[:].bitcast(F32)
+        for u in range(2):
+            nc.tensor.transpose(bt[:, u * P:(u + 1) * P], b_words[:, u:256:2], ident[:])
+        bias = consts.tile([P, 48], F32)
+        nc.vector.tensor_copy(
+            out=bias[:].rearrange("p (h u e) -> p h u e", h=12, u=2),
+            in_=bt[:, 0:256].bitcast(BF16).rearrange("p (u r e) -> p r u e", u=2, e=2)[:, 0:12],
+        )
+
+        xw = x_raw[:].bitcast(F32).rearrange("p (b r w) -> p b r w", b=2, r=3)
+        xg = consts.tile([P, 6144], BF16, align_bytes=64)
+        xg_w = xg[:].bitcast(F32).rearrange("p (c n f u) -> p c n f u", c=2, n=48, f=16)
+        xc = consts.tile([P, 1536], U32, align_bytes=64)
+        xs = consts.tile([P, 1536], U8, align_bytes=64)
+
+        def prep_x(b):
+            for r in range(3):
+                xt = ps_t.tile([P, 512], F32, tag="t")
+                xt_v = xt[:].rearrange("p (q t) -> p q t", q=4)
+                for q in range(4):
+                    lo = 256 * (q // 2) + q % 2
+                    nc.tensor.transpose(xt_v[:, q, :], xw[:, b, r, lo:256 * (q // 2 + 1):2], ident[:])
+                for c in range(2):
+                    copy_on(
+                        "v" if c == 0 else "s",
+                        xg_w[:, c, b * 24 + r:(b + 1) * 24:3, :, :],
+                        xt_v[:, 2 * c:2 * c + 2, :].rearrange("p u (f a) -> p a f u", a=8),
+                    )
+
+        def quant_x(b):
+            for c in range(2):
+                quant(xg, xc, xs, c * 3072 + b * 1536, 1024)
+                quant(xg, xc, xs, c * 3072 + b * 1536 + 1024, 512)
+
+        def regroup(h):
+            engines = REGROUP_ENGINES.get(h, REGROUP_DEFAULT)
+            wg = wg_p.tile([P, 4096], BF16, align_bytes=64)
+            dst = wg[:].rearrange("p (c t q i j) -> p c t q j i", c=2, t=4, q=32, i=4, j=4)
+            src = wraw[h][:].rearrange("p (c j q i t) -> p c t q j i", c=2, j=4, q=32, i=4, t=4)
+            for n in range(8):
+                copy_on(engines[n // 2], dst[:, n // 4, n % 4], src[:, n // 4, n % 4])
+            wgs[h] = wg
+
+        def quant_w(h, pieces):
+            wc = wq_p.tile([P, 1024], U32, align_bytes=64)
+            ws = wq_p.tile([P, 1024], U8, align_bytes=64)
+            for n in range(pieces):
+                quant(wgs[h], wc, ws, n * (4096 // pieces), 4096 // pieces)
+            wcs[h] = (wc, ws)
+
+        def quant_w_whole(h):
+            quant_w(h, 1)
+
+        def k_transposes(h):
+            kw = kraw[h][:].bitcast(F32).rearrange("p (i w) -> p i w", i=6)
+            kts[h] = []
+            for jj in range(3):
+                kt = ps_t.tile([P, 512], F32, tag="t")
+                kt_v = kt[:].rearrange("p (i u r) -> p i u r", i=2, u=2)
+                for ii in range(2):
+                    for u in range(2):
+                        nc.tensor.transpose(kt_v[:, ii, u, :], kw[:, 2 * jj + ii, u:256:2], ident[:])
+                kts[h].append(kt_v)
+
+        def k_evac(h):
+            kg = kg_p.tile([P, 3072], BF16, align_bytes=64)
+            kg_w = kg[:].bitcast(F32).rearrange("p (i r u) -> p i r u", i=6, u=2)
+            for jj in range(3):
+                nc.scalar.copy(out=kg_w[:, 2 * jj:2 * jj + 2], in_=kts[h][jj].rearrange("p i u r -> p i r u"))
+            kgs[h] = kg
+
+        def quant_k(h):
+            kc = kq_p.tile([P, 768], U32, align_bytes=64)
+            ks = kq_p.tile([P, 768], U8, align_bytes=64)
+            quant(kgs[h], kc, ks, 0, 2048)
+            quant(kgs[h], kc, ks, 2048, 1024)
+            kcs[h] = (kc, ks)
+
+        def mm(h, i):
+            wc, ws = wcs[h]
+            y = ps_y.tile([P, 512], F32, tag="y")
+            yv = y[:].rearrange("p (j r) -> p j r", j=4)
+            for j in range(4):
+                for c in range(2):
+                    mx(yv[:, j, :], wc, ws, c * 512 + j * P, xc, xs, c * 768 + i * P, c == 0, c == 1)
+            ys[(h, i)] = y
+
+        def ev(h, i):
+            if h not in qgs:
+                qg = qg_p.tile([P, 3072], BF16, align_bytes=64)
+                qc = qq_p.tile([P, 768], U32, align_bytes=64)
+                qs = qq_p.tile([P, 768], U8, align_bytes=64)
+                qgs[h] = qg
+                qcs[h] = (qc, qs)
+            via = SG_FIRST if h == 0 else SG_LAST if h == LAST else SG_TILES
+            y_rj = ys[(h, i)][:].rearrange("p (j r) -> p r j", j=4)
+            q_rj = qgs[h][:, i * 512:(i + 1) * 512].rearrange("p (r j) -> p r j", j=4)
+            b_rj = bias[:, h * 4:(h + 1) * 4].unsqueeze(1).to_broadcast([P, P, 4])
+            if i in via:
+                yf = yf_p.tile([P, 512], F32)
+                yf_rj = yf[:].rearrange("p (r j) -> p r j", j=4)
+                nc.scalar.copy(out=yf_rj, in_=y_rj)
+                nc.gpsimd.tensor_tensor(out=q_rj, in0=yf_rj, in1=b_rj, op=ALU.add)
+            else:
+                nc.vector.tensor_tensor(out=q_rj, in0=y_rj, in1=b_rj, op=ALU.add)
+
+        def quant_q(h, lo, width):
+            quant(qgs[h], qcs[h][0], qcs[h][1], lo, width)
+
+        def quant_q_a(h):
+            quant_q(h, 0, 2048)
+
+        def quant_q_b(h):
+            quant_q(h, 2048, 1024)
+
+        def s2b(h, b):
+            qc, qs = qcs[h]
+            kc, ks = kcs[h]
+            sc = ps_s.tile([P, 384], F32, tag="s")
+            sc_v = sc[:].rearrange("p (s c) -> p s c", s=3)
+            for s in range(3):
+                i = 3 * b + s
+                mx(sc_v[:, s, :], qc, qs, i * P, kc, ks, i * P, True, False)
+                mx(sc_v[:, s, :], mask_c, mask_s, 0, mask_c, mask_s, P, False, True)
+            scs[(h, b)] = sc
+
+        def s2(h):
+            s2b(h, 0)
+            s2b(h, 1)
+
+        stage = {1: [], 2: [], 3: [], 4: [], 5: []}
+        extracted = set()
+
+        def ex(h, b):
+            n = [m for m in range(len(BATCHES)) if BATCHES[m][0] <= h < BATCHES[m][1]][0]
+            h0, h1 = BATCHES[n]
+            if n not in zts:
+                zt = sm_p.tile([P, 384], F32)
+                zts[n] = zt
+            lo = b * (h1 - h0) * 48 + (h - h0) * 48
+            nc.vector.tensor_reduce(
+                out=zts[n][:, lo:lo + 48].rearrange("p (t g) -> p t g", g=16),
+                in_=scs[(h, b)][:].rearrange("p (s a g) -> p s g a", s=3, a=8),
+                axis=AX.X,
+                op=ALU.max,
+            )
+            extracted.add((h, b))
+            if h == h1 - 1 and (h, 1 - b) in extracted:
+                stage[1].append(n)
+
+        out_v = out.rearrange("b h (s a) f g -> b (h s) (a f) g", s=3)
+
+        def softmax_stage(kk):
+            for n in stage[kk]:
+                h0, h1 = BATCHES[n]
+                groups = (h1 - h0) * 6
+                cols = groups * 16
+                eng = nc.vector if h1 == HEADS else nc.gpsimd
+                if kk == 1:
+                    mxs = sm_p.tile([P, 24], F32)
+                    mxss[n] = mxs
+                    nc.vector.tensor_reduce(out=mxs[:, 0:groups], in_=zts[n][:, 0:cols].rearrange("p (t g) -> p t g", g=16), axis=AX.X, op=ALU.max)
+                elif kk == 2:
+                    zg = zts[n][:, 0:cols].rearrange("p (t g) -> p t g", g=16)
+                    eng.tensor_tensor(out=zg, in0=zg, in1=mxss[n][:, 0:groups].unsqueeze(2).to_broadcast([P, groups, 16]), op=ALU.subtract)
+                elif kk == 3:
+                    et = sm_p.tile([P, 384], F32)
+                    ets[n] = et
+                    nc.scalar.activation(out=et[:, 0:cols], in_=zts[n][:, 0:cols], func=ACT.Exp, scale=SCALE)
+                elif kk == 4:
+                    eg = ets[n][:, 0:cols].rearrange("p (t g) -> p t g", g=16)
+                    sums = sm_p.tile([P, 24], F32)
+                    nc.vector.tensor_reduce(out=sums[:, 0:groups], in_=eg, axis=AX.X, op=ALU.add)
+                    rec = sm_p.tile([P, 24], F32)
+                    recs[n] = rec
+                    nc.vector.reciprocal(out=rec[:, 0:groups], in_=sums[:, 0:groups])
+                else:
+                    eg = ets[n][:, 0:cols].rearrange("p (t g) -> p t g", g=16)
+                    eng.tensor_tensor(out=eg, in0=eg, in1=recs[n][:, 0:groups].unsqueeze(2).to_broadcast([P, groups, 16]), op=ALU.mult)
+                    eb = ets[n][:, 0:cols].rearrange("p (b t g) -> p b t g", b=2, g=16)
+                    for b in range(2):
+                        nc.sync.dma_start(out=out_v[b, h0 * 3:h1 * 3].rearrange("t p g -> p t g"), in_=eb[:, b])
+                if kk < 5:
+                    stage[kk + 1].append(n)
+            stage[kk] = []
+
+        prep_x(0)
+        quant_x(0)
+        regroup(0)
+        quant_w(0, 2)
+        prep_x(1)
+        quant_x(1)
+        regroup(1)
+
+        emit = {
+            "lw": load_w, "lk": load_k, "mm": mm, "e": ev, "rg": regroup, "qw": quant_w_whole,
+            "kt": k_transposes, "ke": k_evac, "qk": quant_k, "qq": quant_q, "qqa": quant_q_a, "qqb": quant_q_b,
+            "s2": s2, "s2b": s2b, "ex": ex,
+        }
+        for h in range(HEADS):
+            steps = FIRST_STEPS if h == 0 else LAST_STEPS if h == LAST else STEADY_STEPS
+            for step in steps:
+                if step[0] == "sm":
+                    softmax_stage(step[1])
+                elif 0 <= h + step[1] < HEADS:
+                    emit[step[0]](h + step[1], *step[2:])

@@ -19,105 +19,6 @@ FLOPS = 2 * 768 * 1024 * 6144 + 2 * 576 * 16 * 16 * 512
 SCALE = 1.0 / 96.0
 BIG = 2.0 ** 100
 BATCHES = ((0, 4), (4, 8), (8, 11), (11, 12))
-REGROUP_ENGINES = {0: "vsvs", 1: "sssg", 2: "sgsg"}
-REGROUP_DEFAULT = "sssg"
-SG_FIRST = ()
-SG_TILES = (0, 1)
-SG_LAST = (0, 1)
-STEADY_STEPS = (
-    ("qw", 1),
-    ("mm", 0, 0),
-    ("mm", 0, 1),
-    ("e", 0, 0),
-    ("mm", 0, 2),
-    ("e", 0, 1),
-    ("mm", 0, 5),
-    ("rg", 2),
-    ("e", 0, 2),
-    ("lw", 4),
-    ("sm", 4),
-    ("mm", 0, 4),
-    ("s2", -1),
-    ("mm", 0, 3),
-    ("ex", -1, 0),
-    ("sm", 1),
-    ("sm", 5),
-    ("e", 0, 4),
-    ("sm", 3),
-    ("kt", 0),
-    ("e", 0, 5),
-    ("lk", 2),
-    ("e", 0, 3),
-    ("ex", -1, 1),
-    ("qqb", 0),
-    ("sm", 2),
-    ("qqa", 0),
-    ("ke", 0),
-    ("qk", 0),
-)
-FIRST_STEPS = (
-    ("mm", 0, 0),
-    ("e", 0, 0),
-    ("mm", 0, 2),
-    ("mm", 0, 1),
-    ("e", 0, 1),
-    ("mm", 0, 3),
-    ("e", 0, 2),
-    ("lk", 2),
-    ("mm", 0, 5),
-    ("e", 0, 3),
-    ("qw", 1),
-    ("mm", 0, 4),
-    ("e", 0, 5),
-    ("rg", 2),
-    ("kt", 0),
-    ("e", 0, 4),
-    ("ke", 0),
-    ("qqb", 0),
-    ("qqa", 0),
-    ("qk", 0),
-    ("lw", 4),
-)
-LAST_STEPS = (
-    ("sm", 4),
-    ("mm", 0, 1),
-    ("mm", 0, 0),
-    ("mm", 0, 2),
-    ("e", 0, 2),
-    ("e", 0, 0),
-    ("s2", -1),
-    ("ex", -1, 1),
-    ("ex", -1, 0),
-    ("sm", 1),
-    ("e", 0, 1),
-    ("mm", 0, 5),
-    ("sm", 5),
-    ("e", 0, 5),
-    ("mm", 0, 3),
-    ("e", 0, 3),
-    ("sm", 2),
-    ("mm", 0, 4),
-    ("kt", 0),
-    ("e", 0, 4),
-    ("ke", 0),
-    ("qq", 0, 0, 1024),
-    ("qq", 0, 2560, 512),
-    ("qq", 0, 1024, 1024),
-    ("qk", 0),
-    ("s2b", 0, 0),
-    ("sm", 3),
-    ("qq", 0, 2048, 512),
-    ("sm", 4),
-    ("ex", 0, 0),
-    ("sm", 5),
-    ("s2b", 0, 1),
-    ("ex", 0, 1),
-    ("sm", 1),
-    ("sm", 2),
-    ("sm", 3),
-    ("sm", 4),
-    ("sm", 5),
-)
 
 
 def tile_dividedspacetimeattention_pa_kernel(tc, x, Wq, bq, k, out):
@@ -125,21 +26,21 @@ def tile_dividedspacetimeattention_pa_kernel(tc, x, Wq, bq, k, out):
     with ExitStack() as ctx:
         consts = ctx.enter_context(tc.tile_pool(name="consts", bufs=1))
         wraw_p = ctx.enter_context(tc.tile_pool(name="wraw", bufs=4))
-        kraw_p = ctx.enter_context(tc.tile_pool(name="kraw", bufs=3))
+        kraw_p = ctx.enter_context(tc.tile_pool(name="kraw", bufs=4))
         wg_p = ctx.enter_context(tc.tile_pool(name="wg", bufs=3))
         wq_p = ctx.enter_context(tc.tile_pool(name="wq", bufs=2))
         kg_p = ctx.enter_context(tc.tile_pool(name="kg", bufs=2))
         kq_p = ctx.enter_context(tc.tile_pool(name="kq", bufs=2))
         qg_p = ctx.enter_context(tc.tile_pool(name="qg", bufs=2))
         qq_p = ctx.enter_context(tc.tile_pool(name="qq", bufs=2))
-        yf_p = ctx.enter_context(tc.tile_pool(name="yf", bufs=2))
+        yp_p = ctx.enter_context(tc.tile_pool(name="yp", bufs=2))
         sm_p = ctx.enter_context(tc.tile_pool(name="sm", bufs=2))
         ps_y = ctx.enter_context(tc.psum_pool(name="psy", bufs=3))
         ps_t = ctx.enter_context(tc.psum_pool(name="pst", bufs=3))
         ps_s = ctx.enter_context(tc.psum_pool(name="pss", bufs=2))
         ctx.enter_context(tc.manual_schedule())
 
-        wraw, kraw, wgs, wcs, kgs, kcs, qgs, qcs, ys, yfs, kts, scs = {}, {}, {}, {}, {}, {}, {}, {}, {}, {}, {}, {}
+        wraw, kraw, wgs, wcs, kgs, kcs, qgs, qcs, ys, yps, kts, scs = {}, {}, {}, {}, {}, {}, {}, {}, {}, {}, {}, {}
         zts, ets, mxss, recs = {}, {}, {}, {}
 
         def copy_on(eng, dst, src):
@@ -215,6 +116,8 @@ def tile_dividedspacetimeattention_pa_kernel(tc, x, Wq, bq, k, out):
         load_k(0)
         load_w(3)
         load_k(1)
+        load_k(2)
+        load_k(3)
 
         mv = mask_in[:].rearrange("p (o a f j) -> p o a f j", o=2, a=8, f=16)
         eye8 = ident[:, 0:8].unsqueeze(2).to_broadcast([P, 8, 16])
@@ -259,14 +162,13 @@ def tile_dividedspacetimeattention_pa_kernel(tc, x, Wq, bq, k, out):
                 quant(xg, xc, xs, c * 3072 + b * 1536, 1024)
                 quant(xg, xc, xs, c * 3072 + b * 1536 + 1024, 512)
 
-        def regroup(h):
-            engines = REGROUP_ENGINES.get(h, REGROUP_DEFAULT)
-            wg = wg_p.tile([P, 4096], BF16, align_bytes=64)
-            dst = wg[:].rearrange("p (c t q i j) -> p c t q j i", c=2, t=4, q=32, i=4, j=4)
+        def regroup(h, n, eng):
+            if h not in wgs:
+                wg = wg_p.tile([P, 4096], BF16, align_bytes=64)
+                wgs[h] = wg
+            dst = wgs[h][:].rearrange("p (c t q i j) -> p c t q j i", c=2, t=4, q=32, i=4, j=4)
             src = wraw[h][:].rearrange("p (c j q i t) -> p c t q j i", c=2, j=4, q=32, i=4, t=4)
-            for n in range(8):
-                copy_on(engines[n // 2], dst[:, n // 4, n % 4], src[:, n // 4, n % 4])
-            wgs[h] = wg
+            copy_on(eng, dst[:, n // 4, n % 4], src[:, n // 4, n % 4])
 
         def quant_w(h, pieces):
             wc = wq_p.tile([P, 1024], U32, align_bytes=64)
@@ -274,9 +176,6 @@ def tile_dividedspacetimeattention_pa_kernel(tc, x, Wq, bq, k, out):
             for n in range(pieces):
                 quant(wgs[h], wc, ws, n * (4096 // pieces), 4096 // pieces)
             wcs[h] = (wc, ws)
-
-        def quant_w_whole(h):
-            quant_w(h, 1)
 
         def k_transposes(h):
             kw = kraw[h][:].bitcast(F32).rearrange("p (i w) -> p i w", i=6)
@@ -292,9 +191,9 @@ def tile_dividedspacetimeattention_pa_kernel(tc, x, Wq, bq, k, out):
         def k_evac(h):
             kg = kg_p.tile([P, 3072], BF16, align_bytes=64)
             kg_w = kg[:].bitcast(F32).rearrange("p (i r u) -> p i r u", i=6, u=2)
+            kgs[h] = kg
             for jj in range(3):
                 nc.scalar.copy(out=kg_w[:, 2 * jj:2 * jj + 2], in_=kts[h][jj].rearrange("p i u r -> p i r u"))
-            kgs[h] = kg
 
         def quant_k(h):
             kc = kq_p.tile([P, 768], U32, align_bytes=64)
@@ -312,33 +211,34 @@ def tile_dividedspacetimeattention_pa_kernel(tc, x, Wq, bq, k, out):
                     mx(yv[:, j, :], wc, ws, c * 512 + j * P, xc, xs, c * 768 + i * P, c == 0, c == 1)
             ys[(h, i)] = y
 
+        def new_q(h):
+            qg = qg_p.tile([P, 3072], BF16, align_bytes=64)
+            qc = qq_p.tile([P, 768], U32, align_bytes=64)
+            qs = qq_p.tile([P, 768], U8, align_bytes=64)
+            qgs[h] = qg
+            qcs[h] = (qc, qs)
+
         def ev(h, i):
-            if h not in qgs:
-                qg = qg_p.tile([P, 3072], BF16, align_bytes=64)
-                qc = qq_p.tile([P, 768], U32, align_bytes=64)
-                qs = qq_p.tile([P, 768], U8, align_bytes=64)
-                qgs[h] = qg
-                qcs[h] = (qc, qs)
-            via = SG_FIRST if h == 0 else SG_LAST if h == LAST else SG_TILES
             y_rj = ys[(h, i)][:].rearrange("p (j r) -> p r j", j=4)
             q_rj = qgs[h][:, i * 512:(i + 1) * 512].rearrange("p (r j) -> p r j", j=4)
             b_rj = bias[:, h * 4:(h + 1) * 4].unsqueeze(1).to_broadcast([P, P, 4])
-            if i in via:
-                yf = yf_p.tile([P, 512], F32)
-                yf_rj = yf[:].rearrange("p (r j) -> p r j", j=4)
-                nc.scalar.copy(out=yf_rj, in_=y_rj)
-                nc.gpsimd.tensor_tensor(out=q_rj, in0=yf_rj, in1=b_rj, op=ALU.add)
-            else:
-                nc.vector.tensor_tensor(out=q_rj, in0=y_rj, in1=b_rj, op=ALU.add)
+            nc.vector.tensor_tensor(out=q_rj, in0=y_rj, in1=b_rj, op=ALU.add)
+
+        def ev_planes(h, i):
+            yp = yp_p.tile([P, 512], BF16)
+            yps[(h, i)] = yp
+            for j in range(4):
+                nc.scalar.activation(
+                    out=yp[:, j * P:(j + 1) * P], in_=ys[(h, i)][:, j * P:(j + 1) * P],
+                    func=ACT.Identity, bias=bias[:, h * 4 + j:h * 4 + j + 1], scale=1.0,
+                )
+
+        def ev_weave(h, i):
+            q_rj = qgs[h][:, i * 512:(i + 1) * 512].rearrange("p (r j) -> p r j", j=4)
+            copy_on("g", q_rj, yps[(h, i)][:].rearrange("p (j r) -> p r j", j=4))
 
         def quant_q(h, lo, width):
             quant(qgs[h], qcs[h][0], qcs[h][1], lo, width)
-
-        def quant_q_a(h):
-            quant_q(h, 0, 2048)
-
-        def quant_q_b(h):
-            quant_q(h, 2048, 1024)
 
         def s2b(h, b):
             qc, qs = qcs[h]
@@ -351,15 +251,11 @@ def tile_dividedspacetimeattention_pa_kernel(tc, x, Wq, bq, k, out):
                 mx(sc_v[:, s, :], mask_c, mask_s, 0, mask_c, mask_s, P, False, True)
             scs[(h, b)] = sc
 
-        def s2(h):
-            s2b(h, 0)
-            s2b(h, 1)
-
-        stage = {1: [], 2: [], 3: [], 4: [], 5: []}
-        extracted = set()
+        def batch_of(h):
+            return [m for m in range(len(BATCHES)) if BATCHES[m][0] <= h < BATCHES[m][1]][0]
 
         def ex(h, b):
-            n = [m for m in range(len(BATCHES)) if BATCHES[m][0] <= h < BATCHES[m][1]][0]
+            n = batch_of(h)
             h0, h1 = BATCHES[n]
             if n not in zts:
                 zt = sm_p.tile([P, 384], F32)
@@ -371,63 +267,129 @@ def tile_dividedspacetimeattention_pa_kernel(tc, x, Wq, bq, k, out):
                 axis=AX.X,
                 op=ALU.max,
             )
-            extracted.add((h, b))
-            if h == h1 - 1 and (h, 1 - b) in extracted:
-                stage[1].append(n)
 
         out_v = out.rearrange("b h (s a) f g -> b (h s) (a f) g", s=3)
 
-        def softmax_stage(kk):
-            for n in stage[kk]:
-                h0, h1 = BATCHES[n]
-                groups = (h1 - h0) * 6
-                cols = groups * 16
-                eng = nc.vector if h1 == HEADS else nc.gpsimd
-                if kk == 1:
-                    mxs = sm_p.tile([P, 24], F32)
-                    mxss[n] = mxs
-                    nc.vector.tensor_reduce(out=mxs[:, 0:groups], in_=zts[n][:, 0:cols].rearrange("p (t g) -> p t g", g=16), axis=AX.X, op=ALU.max)
-                elif kk == 2:
-                    zg = zts[n][:, 0:cols].rearrange("p (t g) -> p t g", g=16)
-                    eng.tensor_tensor(out=zg, in0=zg, in1=mxss[n][:, 0:groups].unsqueeze(2).to_broadcast([P, groups, 16]), op=ALU.subtract)
-                elif kk == 3:
-                    et = sm_p.tile([P, 384], F32)
-                    ets[n] = et
-                    nc.scalar.activation(out=et[:, 0:cols], in_=zts[n][:, 0:cols], func=ACT.Exp, scale=SCALE)
-                elif kk == 4:
-                    eg = ets[n][:, 0:cols].rearrange("p (t g) -> p t g", g=16)
-                    sums = sm_p.tile([P, 24], F32)
-                    nc.vector.tensor_reduce(out=sums[:, 0:groups], in_=eg, axis=AX.X, op=ALU.add)
-                    rec = sm_p.tile([P, 24], F32)
-                    recs[n] = rec
-                    nc.vector.reciprocal(out=rec[:, 0:groups], in_=sums[:, 0:groups])
-                else:
-                    eg = ets[n][:, 0:cols].rearrange("p (t g) -> p t g", g=16)
-                    eng.tensor_tensor(out=eg, in0=eg, in1=recs[n][:, 0:groups].unsqueeze(2).to_broadcast([P, groups, 16]), op=ALU.mult)
-                    eb = ets[n][:, 0:cols].rearrange("p (b t g) -> p b t g", b=2, g=16)
-                    for b in range(2):
-                        nc.sync.dma_start(out=out_v[b, h0 * 3:h1 * 3].rearrange("t p g -> p t g"), in_=eb[:, b])
-                if kk < 5:
-                    stage[kk + 1].append(n)
-            stage[kk] = []
+        def softmax_stage(n, kk):
+            h0, h1 = BATCHES[n]
+            groups = (h1 - h0) * 6
+            cols = groups * 16
+            eng = nc.vector if h1 == HEADS else nc.gpsimd
+            if kk == 1:
+                mxs = sm_p.tile([P, 24], F32)
+                mxss[n] = mxs
+                nc.vector.tensor_reduce(out=mxs[:, 0:groups], in_=zts[n][:, 0:cols].rearrange("p (t g) -> p t g", g=16), axis=AX.X, op=ALU.max)
+            elif kk == 2:
+                zg = zts[n][:, 0:cols].rearrange("p (t g) -> p t g", g=16)
+                eng.tensor_tensor(out=zg, in0=zg, in1=mxss[n][:, 0:groups].unsqueeze(2).to_broadcast([P, groups, 16]), op=ALU.subtract)
+            elif kk == 3:
+                et = sm_p.tile([P, 384], F32)
+                ets[n] = et
+                nc.scalar.activation(out=et[:, 0:cols], in_=zts[n][:, 0:cols], func=ACT.Exp, scale=SCALE)
+            elif kk == 4:
+                eg = ets[n][:, 0:cols].rearrange("p (t g) -> p t g", g=16)
+                sums = sm_p.tile([P, 24], F32)
+                nc.vector.tensor_reduce(out=sums[:, 0:groups], in_=eg, axis=AX.X, op=ALU.add)
+                rec = sm_p.tile([P, 24], F32)
+                recs[n] = rec
+                nc.vector.reciprocal(out=rec[:, 0:groups], in_=sums[:, 0:groups])
+            else:
+                eg = ets[n][:, 0:cols].rearrange("p (t g) -> p t g", g=16)
+                eng.tensor_tensor(out=eg, in0=eg, in1=recs[n][:, 0:groups].unsqueeze(2).to_broadcast([P, groups, 16]), op=ALU.mult)
+                eb = ets[n][:, 0:cols].rearrange("p (b t g) -> p b t g", b=2, g=16)
+                for b in range(2):
+                    nc.sync.dma_start(out=out_v[b, h0 * 3:h1 * 3].rearrange("t p g -> p t g"), in_=eb[:, b])
 
         prep_x(0)
         quant_x(0)
-        regroup(0)
+        for n in range(8):
+            regroup(0, n, "vvssvvss"[n])
         quant_w(0, 2)
+        load_w(4)
         prep_x(1)
         quant_x(1)
-        regroup(1)
+        for n in range(8):
+            regroup(1, n, "ssssssgg"[n])
+        load_w(5)
+        k_transposes(0)
+        k_evac(0)
 
-        emit = {
-            "lw": load_w, "lk": load_k, "mm": mm, "e": ev, "rg": regroup, "qw": quant_w_whole,
-            "kt": k_transposes, "ke": k_evac, "qk": quant_k, "qq": quant_q, "qqa": quant_q_a, "qqb": quant_q_b,
-            "s2": s2, "s2b": s2b, "ex": ex,
-        }
-        for h in range(HEADS):
-            steps = FIRST_STEPS if h == 0 else LAST_STEPS if h == LAST else STEADY_STEPS
-            for step in steps:
-                if step[0] == "sm":
-                    softmax_stage(step[1])
-                elif 0 <= h + step[1] < HEADS:
-                    emit[step[0]](h + step[1], *step[2:])
+        def on(h):
+            return 0 <= h < HEADS
+
+        for h in range(HEADS - 1):
+            done = [n for n in range(len(BATCHES)) if BATCHES[n][1] == h - 2]
+            new_q(h)
+            for i in range(6):
+                mm(h, i)
+                if i in (1,):
+                    ev_planes(h, i)
+                    ev_weave(h, i)
+                else:
+                    ev(h, i)
+                if on(h + 2):
+                    if i < 5:
+                        regroup(h + 2, i, "s")
+                    for n in {1: (6,), 3: (7,)}.get(i, ()):
+                        regroup(h + 2, n, "g")
+                if i in (2, 3) and on(h - 2):
+                    ex(h - 2, i - 2)
+                if i > 0:
+                    for n in done:
+                        softmax_stage(n, i)
+            if on(h + 1):
+                k_transposes(h + 1)
+                quant_w(h + 1, 1)
+                k_evac(h + 1)
+            if on(h + 4):
+                load_k(h + 4)
+            if on(h + 2):
+                regroup(h + 2, 5, "s")
+            if on(h + 6):
+                load_w(h + 6)
+            if on(h - 1):
+                for b in range(2):
+                    s2b(h - 1, b)
+            quant_q(h, 0, 2048)
+            quant_q(h, 2048, 1024)
+            quant_k(h)
+
+        h = LAST
+        new_q(h)
+        for i in range(3):
+            mm(h, i)
+            if i == 0:
+                ev_planes(h, i)
+                ev_weave(h, i)
+            else:
+                ev(h, i)
+            if i > 0:
+                ex(h - 2, i - 1)
+        for b in range(2):
+            s2b(h - 1, b)
+        quant_k(h)
+        for i in range(3, 6):
+            mm(h, i)
+            ev(h, i)
+            if i == 3:
+                quant_q(h, 0, 1024)
+                ex(h - 1, 0)
+            if i == 4:
+                quant_q(h, 1024, 512)
+                ex(h - 1, 1)
+        s2b(h, 0)
+        quant_q(h, 1536, 1024)
+        softmax_stage(2, 1)
+        quant_q(h, 2560, 512)
+        s2b(h, 1)
+        softmax_stage(2, 2)
+        softmax_stage(2, 3)
+        ex(h, 0)
+        softmax_stage(2, 4)
+        ex(h, 1)
+        softmax_stage(3, 1)
+        softmax_stage(3, 2)
+        softmax_stage(3, 3)
+        softmax_stage(2, 5)
+        softmax_stage(3, 4)
+        softmax_stage(3, 5)

@@ -18,7 +18,7 @@ LAST = HEADS - 1
 FLOPS = 2 * 768 * 1024 * 6144 + 2 * 576 * 16 * 16 * 512
 SCALE = 1.0 / 96.0
 BIG = 2.0 ** 100
-BATCHES = ((0, 4), (4, 8), (8, 11), (11, 12))
+BATCHES = ((0, 4), (4, 8), (8, 10), (10, 12))
 
 
 def tile_dividedspacetimeattention_pa_kernel(tc, x, Wq, bq, k, out):
@@ -105,19 +105,20 @@ def tile_dividedspacetimeattention_pa_kernel(tc, x, Wq, bq, k, out):
         xr_v = x_raw[:].rearrange("p (b r c) -> p b r c", b=2, r=3)
 
         def load_x(b):
-            nc.sync.dma_start(out=xr_v[:, b], in_=x[b].rearrange("(p r) c -> p r c", r=3))
+            xb = x[b].rearrange("(p r) c -> p r c", r=3)
+            for r in range(3):
+                nc.sync.dma_start(out=xr_v[:, b, r], in_=xb[:, r])
 
+        load_w(0)
         load_x(0)
         nc.sync.dma_start(out=b_raw[0:12, :], in_=bq.rearrange("(r c) -> r c", c=512))
-        load_w(0)
         load_x(1)
         load_w(1)
-        load_w(2)
         load_k(0)
-        load_w(3)
+        load_w(2)
         load_k(1)
+        load_w(3)
         load_k(2)
-        load_k(3)
 
         mv = mask_in[:].rearrange("p (o a f j) -> p o a f j", o=2, a=8, f=16)
         eye8 = ident[:, 0:8].unsqueeze(2).to_broadcast([P, 8, 16])
@@ -127,15 +128,17 @@ def tile_dividedspacetimeattention_pa_kernel(tc, x, Wq, bq, k, out):
         mask_s = consts.tile([P, 256], U8, align_bytes=64)
         quant(mask_in, mask_c, mask_s, 0, 1024)
 
-        bt = ps_t.tile([P, 512], F32, tag="t")
-        b_words = b_raw[:].bitcast(F32)
-        for u in range(2):
-            nc.tensor.transpose(bt[:, u * P:(u + 1) * P], b_words[:, u:256:2], ident[:])
         bias = consts.tile([P, 48], F32)
-        nc.vector.tensor_copy(
-            out=bias[:].rearrange("p (h u e) -> p h u e", h=12, u=2),
-            in_=bt[:, 0:256].bitcast(BF16).rearrange("p (u r e) -> p r u e", u=2, e=2)[:, 0:12],
-        )
+
+        def prep_bias():
+            bt = ps_t.tile([P, 512], F32, tag="t")
+            b_words = b_raw[:].bitcast(F32)
+            for u in range(2):
+                nc.tensor.transpose(bt[:, u * P:(u + 1) * P], b_words[:, u:256:2], ident[:])
+            nc.vector.tensor_copy(
+                out=bias[:].rearrange("p (h u e) -> p h u e", h=12, u=2),
+                in_=bt[:, 0:256].bitcast(BF16).rearrange("p (u r e) -> p r u e", u=2, e=2)[:, 0:12],
+            )
 
         xw = x_raw[:].bitcast(F32).rearrange("p (b r w) -> p b r w", b=2, r=3)
         xg = consts.tile([P, 6144], BF16, align_bytes=64)
@@ -152,7 +155,7 @@ def tile_dividedspacetimeattention_pa_kernel(tc, x, Wq, bq, k, out):
                     nc.tensor.transpose(xt_v[:, q, :], xw[:, b, r, lo:256 * (q // 2 + 1):2], ident[:])
                 for c in range(2):
                     copy_on(
-                        "v" if c == 0 else "s",
+                        "v" if b == 1 and c == 0 else "s",
                         xg_w[:, c, b * 24 + r:(b + 1) * 24:3, :, :],
                         xt_v[:, 2 * c:2 * c + 2, :].rearrange("p u (f a) -> p a f u", a=8),
                     )
@@ -166,9 +169,14 @@ def tile_dividedspacetimeattention_pa_kernel(tc, x, Wq, bq, k, out):
             if h not in wgs:
                 wg = wg_p.tile([P, 4096], BF16, align_bytes=64)
                 wgs[h] = wg
-            dst = wgs[h][:].rearrange("p (c t q i j) -> p c t q j i", c=2, t=4, q=32, i=4, j=4)
-            src = wraw[h][:].rearrange("p (c j q i t) -> p c t q j i", c=2, j=4, q=32, i=4, t=4)
-            copy_on(eng, dst[:, n // 4, n % 4], src[:, n // 4, n % 4])
+            c, q0 = n // 2, 32 * (n % 2)
+            dst = wgs[h][:].rearrange("p (c t q i j) -> p c q j i t", c=2, t=4, q=64, i=2, j=4)
+            src = wraw[h][:].rearrange("p (c j q i t) -> p c q j i t", c=2, j=4, q=64, i=2, t=4)
+            if eng == "g":
+                for t in range(4):
+                    copy_on(eng, dst[:, c, q0:q0 + 32, :, :, t], src[:, c, q0:q0 + 32, :, :, t])
+            else:
+                copy_on(eng, dst[:, c, q0:q0 + 32], src[:, c, q0:q0 + 32])
 
         def quant_w(h, pieces):
             wc = wq_p.tile([P, 1024], U32, align_bytes=64)
@@ -270,81 +278,98 @@ def tile_dividedspacetimeattention_pa_kernel(tc, x, Wq, bq, k, out):
 
         out_v = out.rearrange("b h (s a) f g -> b (h s) (a f) g", s=3)
 
-        def softmax_stage(n, kk):
+        def softmax_stage(n, kk, clip=None):
             h0, h1 = BATCHES[n]
-            groups = (h1 - h0) * 6
-            cols = groups * 16
+            per = (h1 - h0) * 3
+            clips = (0, 1) if clip is None else (clip,)
+            g0, groups = clips[0] * per, len(clips) * per
+            t0, t1 = g0 * 16, (g0 + groups) * 16
             eng = nc.vector if h1 == HEADS else nc.gpsimd
             if kk == 1:
-                mxs = sm_p.tile([P, 24], F32)
-                mxss[n] = mxs
-                nc.vector.tensor_reduce(out=mxs[:, 0:groups], in_=zts[n][:, 0:cols].rearrange("p (t g) -> p t g", g=16), axis=AX.X, op=ALU.max)
+                if n not in mxss:
+                    mxs = sm_p.tile([P, 24], F32)
+                    mxss[n] = mxs
+                nc.vector.tensor_reduce(out=mxss[n][:, g0:g0 + groups], in_=zts[n][:, t0:t1].rearrange("p (t g) -> p t g", g=16), axis=AX.X, op=ALU.max)
             elif kk == 2:
-                zg = zts[n][:, 0:cols].rearrange("p (t g) -> p t g", g=16)
-                eng.tensor_tensor(out=zg, in0=zg, in1=mxss[n][:, 0:groups].unsqueeze(2).to_broadcast([P, groups, 16]), op=ALU.subtract)
+                zg = zts[n][:, t0:t1].rearrange("p (t g) -> p t g", g=16)
+                eng.tensor_tensor(out=zg, in0=zg, in1=mxss[n][:, g0:g0 + groups].unsqueeze(2).to_broadcast([P, groups, 16]), op=ALU.subtract)
             elif kk == 3:
-                et = sm_p.tile([P, 384], F32)
-                ets[n] = et
-                nc.scalar.activation(out=et[:, 0:cols], in_=zts[n][:, 0:cols], func=ACT.Exp, scale=SCALE)
+                if n not in ets:
+                    et = sm_p.tile([P, 384], F32)
+                    ets[n] = et
+                nc.scalar.activation(out=ets[n][:, t0:t1], in_=zts[n][:, t0:t1], func=ACT.Exp, scale=SCALE)
             elif kk == 4:
-                eg = ets[n][:, 0:cols].rearrange("p (t g) -> p t g", g=16)
+                eg = ets[n][:, t0:t1].rearrange("p (t g) -> p t g", g=16)
                 sums = sm_p.tile([P, 24], F32)
                 nc.vector.tensor_reduce(out=sums[:, 0:groups], in_=eg, axis=AX.X, op=ALU.add)
-                rec = sm_p.tile([P, 24], F32)
-                recs[n] = rec
-                nc.vector.reciprocal(out=rec[:, 0:groups], in_=sums[:, 0:groups])
+                if n not in recs:
+                    rec = sm_p.tile([P, 24], F32)
+                    recs[n] = rec
+                nc.vector.reciprocal(out=recs[n][:, g0:g0 + groups], in_=sums[:, 0:groups])
             else:
-                eg = ets[n][:, 0:cols].rearrange("p (t g) -> p t g", g=16)
-                eng.tensor_tensor(out=eg, in0=eg, in1=recs[n][:, 0:groups].unsqueeze(2).to_broadcast([P, groups, 16]), op=ALU.mult)
-                eb = ets[n][:, 0:cols].rearrange("p (b t g) -> p b t g", b=2, g=16)
-                for b in range(2):
-                    nc.sync.dma_start(out=out_v[b, h0 * 3:h1 * 3].rearrange("t p g -> p t g"), in_=eb[:, b])
+                eg = ets[n][:, t0:t1].rearrange("p (t g) -> p t g", g=16)
+                eng.tensor_tensor(out=eg, in0=eg, in1=recs[n][:, g0:g0 + groups].unsqueeze(2).to_broadcast([P, groups, 16]), op=ALU.mult)
+                for b in clips:
+                    nc.sync.dma_start(
+                        out=out_v[b, h0 * 3:h1 * 3].rearrange("t p g -> p t g"),
+                        in_=ets[n][:, b * per * 16:(b + 1) * per * 16].rearrange("p (t g) -> p t g", g=16),
+                    )
 
+        for n in range(4):
+            regroup(0, n, "vsvv"[n])
+        load_w(4)
+        quant_w(0, 2)
         prep_x(0)
         quant_x(0)
-        for n in range(8):
-            regroup(0, n, "vvssvvss"[n])
-        quant_w(0, 2)
-        load_w(4)
         prep_x(1)
+        prep_bias()
         quant_x(1)
-        for n in range(8):
-            regroup(1, n, "ssssssgg"[n])
-        load_w(5)
-        k_transposes(0)
-        k_evac(0)
 
         def on(h):
             return 0 <= h < HEADS
 
         for h in range(HEADS - 1):
-            done = [n for n in range(len(BATCHES)) if BATCHES[n][1] == h - 2]
+            done = [n for n in range(2) if BATCHES[n][1] == h - 2]
+            late = [n for n in range(2) if BATCHES[n][1] == h - 3]
+            for n in done:
+                softmax_stage(n, 1)
+                softmax_stage(n, 2)
+            for n in late:
+                softmax_stage(n, 4)
+                softmax_stage(n, 5)
             new_q(h)
             for i in range(6):
                 mm(h, i)
-                if i in (1,):
+                if h == 0 and i < 4:
+                    for n, eng in (((0, "s"),), ((1, "s"), (2, "v")), (), ((3, "v"),))[i]:
+                        regroup(1, n, eng)
+                if i in (1,) and h > 0:
                     ev_planes(h, i)
                     ev_weave(h, i)
                 else:
                     ev(h, i)
                 if on(h + 2):
-                    if i < 5:
-                        regroup(h + 2, i, "s")
-                    for n in {1: (6,), 3: (7,)}.get(i, ()):
-                        regroup(h + 2, n, "g")
+                    if i in (0, 3) and h > 0:
+                        regroup(h + 2, i // 3, "s")
+                    if i == 1 and h > 0:
+                        regroup(h + 2, 3, "g")
                 if i in (2, 3) and on(h - 2):
                     ex(h - 2, i - 2)
-                if i > 0:
-                    for n in done:
-                        softmax_stage(n, i)
-            if on(h + 1):
-                k_transposes(h + 1)
-                quant_w(h + 1, 1)
-                k_evac(h + 1)
-            if on(h + 4):
-                load_k(h + 4)
+            if h == 0:
+                load_w(5)
+            k_transposes(h)
+            quant_w(h + 1, 1)
+            k_evac(h)
+            for n in done:
+                softmax_stage(n, 3)
+            if on(h + 3):
+                load_k(h + 3)
+            if h == 0:
+                for n in range(2):
+                    regroup(2, n, "s")
+                regroup(2, 3, "g")
             if on(h + 2):
-                regroup(h + 2, 5, "s")
+                regroup(h + 2, 2, "s")
             if on(h + 6):
                 load_w(h + 6)
             if on(h - 1):
@@ -356,40 +381,48 @@ def tile_dividedspacetimeattention_pa_kernel(tc, x, Wq, bq, k, out):
 
         h = LAST
         new_q(h)
+        softmax_stage(1, 4)
+        softmax_stage(1, 5)
         for i in range(3):
             mm(h, i)
-            if i == 0:
-                ev_planes(h, i)
-                ev_weave(h, i)
-            else:
-                ev(h, i)
-            if i > 0:
-                ex(h - 2, i - 1)
+        k_transposes(h)
+        for i in range(3, 6):
+            mm(h, i)
+        ev_planes(h, 1)
+        ev_weave(h, 1)
+        k_evac(h)
+        ev(h, 0)
+        ev(h, 2)
+        ex(h - 2, 0)
+        ex(h - 2, 1)
+        ev(h, 3)
         for b in range(2):
             s2b(h - 1, b)
         quant_k(h)
-        for i in range(3, 6):
-            mm(h, i)
-            ev(h, i)
-            if i == 3:
-                quant_q(h, 0, 1024)
-                ex(h - 1, 0)
-            if i == 4:
-                quant_q(h, 1024, 512)
-                ex(h - 1, 1)
-        s2b(h, 0)
-        quant_q(h, 1536, 1024)
+        quant_q(h, 0, 1024)
+        ev(h, 4)
         softmax_stage(2, 1)
+        quant_q(h, 1024, 512)
+        s2b(h, 0)
+        softmax_stage(2, 2)
+        ev(h, 5)
+        softmax_stage(2, 3)
+        quant_q(h, 1536, 1024)
         quant_q(h, 2560, 512)
         s2b(h, 1)
-        softmax_stage(2, 2)
-        softmax_stage(2, 3)
-        ex(h, 0)
         softmax_stage(2, 4)
-        ex(h, 1)
-        softmax_stage(3, 1)
-        softmax_stage(3, 2)
-        softmax_stage(3, 3)
         softmax_stage(2, 5)
-        softmax_stage(3, 4)
-        softmax_stage(3, 5)
+        for b in range(2):
+            ex(h - 1, b)
+        ex(h, 0)
+        softmax_stage(3, 1, 0)
+        ex(h, 1)
+        softmax_stage(3, 2, 0)
+        softmax_stage(3, 3, 0)
+        softmax_stage(3, 1, 1)
+        softmax_stage(3, 2, 1)
+        softmax_stage(3, 3, 1)
+        softmax_stage(3, 4, 0)
+        softmax_stage(3, 5, 0)
+        softmax_stage(3, 4, 1)
+        softmax_stage(3, 5, 1)

@@ -343,16 +343,10 @@ def tile_dividedspacetimeattention_pa_kernel(tc, x, Wq, bq, k, out):
                 if h == 0 and i < 4:
                     for n, eng in (((0, "s"),), ((1, "s"), (2, "v")), (), ((3, "v"),))[i]:
                         regroup(1, n, eng)
-                if i in (1,) and h > 0:
-                    ev_planes(h, i)
-                    ev_weave(h, i)
-                else:
-                    ev(h, i)
+                ev(h, i)
                 if on(h + 2):
-                    if i in (0, 3) and h > 0:
-                        regroup(h + 2, i // 3, "s")
-                    if i == 1 and h > 0:
-                        regroup(h + 2, 3, "g")
+                    if i in (0, 2, 4) and h > 0:
+                        regroup(h + 2, i // 2, "s")
                 if i in (2, 3) and on(h - 2):
                     ex(h - 2, i - 2)
             if h == 0:
@@ -365,11 +359,10 @@ def tile_dividedspacetimeattention_pa_kernel(tc, x, Wq, bq, k, out):
             if on(h + 3):
                 load_k(h + 3)
             if h == 0:
-                for n in range(2):
+                for n in range(3):
                     regroup(2, n, "s")
-                regroup(2, 3, "g")
             if on(h + 2):
-                regroup(h + 2, 2, "s")
+                regroup(h + 2, 3, "s")
             if on(h + 6):
                 load_w(h + 6)
             if on(h - 1):
@@ -388,11 +381,9 @@ def tile_dividedspacetimeattention_pa_kernel(tc, x, Wq, bq, k, out):
         k_transposes(h)
         for i in range(3, 6):
             mm(h, i)
-        ev_planes(h, 1)
-        ev_weave(h, 1)
         k_evac(h)
-        ev(h, 0)
-        ev(h, 2)
+        for i in range(3):
+            ev(h, i)
         ex(h - 2, 0)
         ex(h - 2, 1)
         ev(h, 3)

@@ -15,6 +15,7 @@ AX = mybir.AxisListType
 P = 128
 HEADS = 12
 LAST = HEADS - 1
+SG_TILES = (2, 4)
 FLOPS = 2 * 768 * 1024 * 6144 + 2 * 576 * 16 * 16 * 512
 SCALE = 1.0 / 96.0
 BIG = 2.0 ** 100
@@ -29,10 +30,8 @@ def tile_dividedspacetimeattention_pa_kernel(tc, x, Wq, bq, k, out):
         kraw_p = ctx.enter_context(tc.tile_pool(name="kraw", bufs=4))
         wg_p = ctx.enter_context(tc.tile_pool(name="wg", bufs=3))
         wq_p = ctx.enter_context(tc.tile_pool(name="wq", bufs=2))
-        kg_p = ctx.enter_context(tc.tile_pool(name="kg", bufs=2))
-        kq_p = ctx.enter_context(tc.tile_pool(name="kq", bufs=2))
-        qg_p = ctx.enter_context(tc.tile_pool(name="qg", bufs=2))
-        qq_p = ctx.enter_context(tc.tile_pool(name="qq", bufs=2))
+        sg_p = ctx.enter_context(tc.tile_pool(name="sg", bufs=2))
+        sq_p = ctx.enter_context(tc.tile_pool(name="sq", bufs=2))
         yp_p = ctx.enter_context(tc.tile_pool(name="yp", bufs=2))
         sm_p = ctx.enter_context(tc.tile_pool(name="sm", bufs=2))
         ps_y = ctx.enter_context(tc.psum_pool(name="psy", bufs=3))
@@ -40,7 +39,7 @@ def tile_dividedspacetimeattention_pa_kernel(tc, x, Wq, bq, k, out):
         ps_s = ctx.enter_context(tc.psum_pool(name="pss", bufs=2))
         ctx.enter_context(tc.manual_schedule())
 
-        wraw, kraw, wgs, wcs, kgs, kcs, qgs, qcs, ys, yps, kts, scs = {}, {}, {}, {}, {}, {}, {}, {}, {}, {}, {}, {}
+        wraw, kraw, wgs, wcs, sgs, sqs, ys, yps, kts, scs = {}, {}, {}, {}, {}, {}, {}, {}, {}, {}
         zts, ets, mxss, recs = {}, {}, {}, {}
 
         def copy_on(eng, dst, src):
@@ -197,18 +196,9 @@ def tile_dividedspacetimeattention_pa_kernel(tc, x, Wq, bq, k, out):
                 kts[h].append(kt_v)
 
         def k_evac(h):
-            kg = kg_p.tile([P, 3072], BF16, align_bytes=64)
-            kg_w = kg[:].bitcast(F32).rearrange("p (i r u) -> p i r u", i=6, u=2)
-            kgs[h] = kg
+            kg_w = sgs[h][:, 3072:6144].bitcast(F32).rearrange("p (i r u) -> p i r u", i=6, u=2)
             for jj in range(3):
                 nc.scalar.copy(out=kg_w[:, 2 * jj:2 * jj + 2], in_=kts[h][jj].rearrange("p i u r -> p i r u"))
-
-        def quant_k(h):
-            kc = kq_p.tile([P, 768], U32, align_bytes=64)
-            ks = kq_p.tile([P, 768], U8, align_bytes=64)
-            quant(kgs[h], kc, ks, 0, 2048)
-            quant(kgs[h], kc, ks, 2048, 1024)
-            kcs[h] = (kc, ks)
 
         def mm(h, i):
             wc, ws = wcs[h]
@@ -219,16 +209,16 @@ def tile_dividedspacetimeattention_pa_kernel(tc, x, Wq, bq, k, out):
                     mx(yv[:, j, :], wc, ws, c * 512 + j * P, xc, xs, c * 768 + i * P, c == 0, c == 1)
             ys[(h, i)] = y
 
-        def new_q(h):
-            qg = qg_p.tile([P, 3072], BF16, align_bytes=64)
-            qc = qq_p.tile([P, 768], U32, align_bytes=64)
-            qs = qq_p.tile([P, 768], U8, align_bytes=64)
-            qgs[h] = qg
-            qcs[h] = (qc, qs)
+        def new_scores(h):
+            sg = sg_p.tile([P, 6144], BF16, align_bytes=64)
+            sc_c = sq_p.tile([P, 1536], U32, align_bytes=64)
+            sc_s = sq_p.tile([P, 1536], U8, align_bytes=64)
+            sgs[h] = sg
+            sqs[h] = (sc_c, sc_s)
 
         def ev(h, i):
             y_rj = ys[(h, i)][:].rearrange("p (j r) -> p r j", j=4)
-            q_rj = qgs[h][:, i * 512:(i + 1) * 512].rearrange("p (r j) -> p r j", j=4)
+            q_rj = sgs[h][:, i * 512:(i + 1) * 512].rearrange("p (r j) -> p r j", j=4)
             b_rj = bias[:, h * 4:(h + 1) * 4].unsqueeze(1).to_broadcast([P, P, 4])
             nc.vector.tensor_tensor(out=q_rj, in0=y_rj, in1=b_rj, op=ALU.add)
 
@@ -242,20 +232,19 @@ def tile_dividedspacetimeattention_pa_kernel(tc, x, Wq, bq, k, out):
                 )
 
         def ev_weave(h, i):
-            q_rj = qgs[h][:, i * 512:(i + 1) * 512].rearrange("p (r j) -> p r j", j=4)
-            copy_on("g", q_rj, yps[(h, i)][:].rearrange("p (j r) -> p r j", j=4))
+            q_w = sgs[h][:, i * 512:(i + 1) * 512].rearrange("p (n r j) -> p n j r", r=8, j=4)
+            copy_on("g", q_w, yps[(h, i)][:].rearrange("p (j n r) -> p n j r", j=4, r=8))
 
-        def quant_q(h, lo, width):
-            quant(qgs[h], qcs[h][0], qcs[h][1], lo, width)
+        def quant_qk(h, lo, width):
+            quant(sgs[h], sqs[h][0], sqs[h][1], lo, width)
 
         def s2b(h, b):
-            qc, qs = qcs[h]
-            kc, ks = kcs[h]
+            qk_c, qk_s = sqs[h]
             sc = ps_s.tile([P, 384], F32, tag="s")
             sc_v = sc[:].rearrange("p (s c) -> p s c", s=3)
             for s in range(3):
                 i = 3 * b + s
-                mx(sc_v[:, s, :], qc, qs, i * P, kc, ks, i * P, True, False)
+                mx(sc_v[:, s, :], qk_c, qk_s, i * P, qk_c, qk_s, 768 + i * P, True, False)
                 mx(sc_v[:, s, :], mask_c, mask_s, 0, mask_c, mask_s, P, False, True)
             scs[(h, b)] = sc
 
@@ -337,13 +326,17 @@ def tile_dividedspacetimeattention_pa_kernel(tc, x, Wq, bq, k, out):
             for n in late:
                 softmax_stage(n, 4)
                 softmax_stage(n, 5)
-            new_q(h)
+            new_scores(h)
             for i in range(6):
                 mm(h, i)
                 if h == 0 and i < 4:
                     for n, eng in (((0, "s"),), ((1, "s"), (2, "v")), (), ((3, "v"),))[i]:
                         regroup(1, n, eng)
-                ev(h, i)
+                if i in SG_TILES and h > 0:
+                    ev_planes(h, i)
+                    ev_weave(h, i)
+                else:
+                    ev(h, i)
                 if on(h + 2):
                     if i in (0, 2, 4) and h > 0:
                         regroup(h + 2, i // 2, "s")
@@ -368,12 +361,11 @@ def tile_dividedspacetimeattention_pa_kernel(tc, x, Wq, bq, k, out):
             if on(h - 1):
                 for b in range(2):
                     s2b(h - 1, b)
-            quant_q(h, 0, 2048)
-            quant_q(h, 2048, 1024)
-            quant_k(h)
+            quant_qk(h, 0, 4096)
+            quant_qk(h, 4096, 2048)
 
         h = LAST
-        new_q(h)
+        new_scores(h)
         softmax_stage(1, 4)
         softmax_stage(1, 5)
         for i in range(3):
@@ -389,17 +381,18 @@ def tile_dividedspacetimeattention_pa_kernel(tc, x, Wq, bq, k, out):
         ev(h, 3)
         for b in range(2):
             s2b(h - 1, b)
-        quant_k(h)
-        quant_q(h, 0, 1024)
+        quant_qk(h, 3072, 2048)
+        quant_qk(h, 5120, 1024)
+        quant_qk(h, 0, 1024)
         ev(h, 4)
         softmax_stage(2, 1)
-        quant_q(h, 1024, 512)
+        quant_qk(h, 1024, 512)
         s2b(h, 0)
         softmax_stage(2, 2)
         ev(h, 5)
         softmax_stage(2, 3)
-        quant_q(h, 1536, 1024)
-        quant_q(h, 2560, 512)
+        quant_qk(h, 1536, 1024)
+        quant_qk(h, 2560, 512)
         s2b(h, 1)
         softmax_stage(2, 4)
         softmax_stage(2, 5)

@@ -15,7 +15,10 @@ AX = mybir.AxisListType
 P = 128
 HEADS = 12
 LAST = HEADS - 1
-SG_TILES = (2, 4)
+SG_TILES = (0, 3)
+LAST_TILES = (0, 3)
+S_SLOTS = (0, 3)
+G_SLOTS = (0, 3)
 FLOPS = 2 * 768 * 1024 * 6144 + 2 * 576 * 16 * 16 * 512
 SCALE = 1.0 / 96.0
 BIG = 2.0 ** 100
@@ -164,7 +167,7 @@ def tile_dividedspacetimeattention_pa_kernel(tc, x, Wq, bq, k, out):
                 quant(xg, xc, xs, c * 3072 + b * 1536, 1024)
                 quant(xg, xc, xs, c * 3072 + b * 1536 + 1024, 512)
 
-        def regroup(h, n, eng):
+        def regroup(h, n, eng, half=0):
             if h not in wgs:
                 wg = wg_p.tile([P, 4096], BF16, align_bytes=64)
                 wgs[h] = wg
@@ -172,8 +175,11 @@ def tile_dividedspacetimeattention_pa_kernel(tc, x, Wq, bq, k, out):
             dst = wgs[h][:].rearrange("p (c t q i j) -> p c q j i t", c=2, t=4, q=64, i=2, j=4)
             src = wraw[h][:].rearrange("p (c j q i t) -> p c q j i t", c=2, j=4, q=64, i=2, t=4)
             if eng == "g":
-                for t in range(4):
-                    copy_on(eng, dst[:, c, q0:q0 + 32, :, :, t], src[:, c, q0:q0 + 32, :, :, t])
+                m0 = 2 * q0
+                g_dst = wgs[h][:].rearrange("p (c t m j) -> p c t m j", c=2, t=4, j=4)
+                g_src = wraw[h][:].rearrange("p (c j m t) -> p c t m j", c=2, j=4, t=4)
+                for t in range(2 * half, 2 * half + 2, 2):
+                    copy_on(eng, g_dst[:, c, t:t + 2, m0:m0 + 64], g_src[:, c, t:t + 2, m0:m0 + 64])
             else:
                 copy_on(eng, dst[:, c, q0:q0 + 32], src[:, c, q0:q0 + 32])
 
@@ -232,11 +238,18 @@ def tile_dividedspacetimeattention_pa_kernel(tc, x, Wq, bq, k, out):
                 )
 
         def ev_weave(h, i):
-            q_w = sgs[h][:, i * 512:(i + 1) * 512].rearrange("p (n r j) -> p n j r", r=8, j=4)
-            copy_on("g", q_w, yps[(h, i)][:].rearrange("p (j n r) -> p n j r", j=4, r=8))
+            q_rj = sgs[h][:, i * 512:(i + 1) * 512].rearrange("p (r j) -> p r j", j=4)
+            copy_on("g", q_rj, yps[(h, i)][:].rearrange("p (j r) -> p r j", j=4))
 
         def quant_qk(h, lo, width):
             quant(sgs[h], sqs[h][0], sqs[h][1], lo, width)
+
+        def evac(h, i):
+            if i in (LAST_TILES if h == LAST else SG_TILES) and h > 0:
+                ev_planes(h, i)
+                ev_weave(h, i)
+            else:
+                ev(h, i)
 
         def s2b(h, b):
             qk_c, qk_s = sqs[h]
@@ -330,16 +343,14 @@ def tile_dividedspacetimeattention_pa_kernel(tc, x, Wq, bq, k, out):
             for i in range(6):
                 mm(h, i)
                 if h == 0 and i < 4:
-                    for n, eng in (((0, "s"),), ((1, "s"), (2, "v")), (), ((3, "v"),))[i]:
+                    for n, eng in (((0, "s"), (1, "s"), (2, "s"), (3, "s")), (), (), ())[i]:
                         regroup(1, n, eng)
-                if i in SG_TILES and h > 0:
-                    ev_planes(h, i)
-                    ev_weave(h, i)
-                else:
-                    ev(h, i)
-                if on(h + 2):
-                    if i in (0, 2, 4) and h > 0:
-                        regroup(h + 2, i // 2, "s")
+                evac(h, i)
+                if h > 0:
+                    if i in S_SLOTS:
+                        regroup(h + 1, 1 + S_SLOTS.index(i), "s")
+                    if i in G_SLOTS:
+                        regroup(h + 1, 3, "g", G_SLOTS.index(i))
                 if i in (2, 3) and on(h - 2):
                     ex(h - 2, i - 2)
             if h == 0:
@@ -351,13 +362,10 @@ def tile_dividedspacetimeattention_pa_kernel(tc, x, Wq, bq, k, out):
                 softmax_stage(n, 3)
             if on(h + 3):
                 load_k(h + 3)
-            if h == 0:
-                for n in range(3):
-                    regroup(2, n, "s")
             if on(h + 2):
-                regroup(h + 2, 3, "s")
-            if on(h + 6):
-                load_w(h + 6)
+                regroup(h + 2, 0, "s")
+            if on(h + 5) and h > 0:
+                load_w(h + 5)
             if on(h - 1):
                 for b in range(2):
                     s2b(h - 1, b)
@@ -373,23 +381,24 @@ def tile_dividedspacetimeattention_pa_kernel(tc, x, Wq, bq, k, out):
         k_transposes(h)
         for i in range(3, 6):
             mm(h, i)
+        evac(h, 0)
         k_evac(h)
-        for i in range(3):
-            ev(h, i)
+        evac(h, 1)
+        evac(h, 2)
         ex(h - 2, 0)
         ex(h - 2, 1)
-        ev(h, 3)
+        evac(h, 3)
         for b in range(2):
             s2b(h - 1, b)
         quant_qk(h, 3072, 2048)
         quant_qk(h, 5120, 1024)
         quant_qk(h, 0, 1024)
-        ev(h, 4)
+        evac(h, 4)
         softmax_stage(2, 1)
         quant_qk(h, 1024, 512)
         s2b(h, 0)
         softmax_stage(2, 2)
-        ev(h, 5)
+        evac(h, 5)
         softmax_stage(2, 3)
         quant_qk(h, 1536, 1024)
         quant_qk(h, 2560, 512)

@@ -18,7 +18,7 @@ LAST = HEADS - 1
 SG_TILES = (0, 3)
 LAST_TILES = (0, 3)
 S_SLOTS = (0, 3)
-G_SLOTS = (0, 3)
+V_SLOT = 0
 FLOPS = 2 * 768 * 1024 * 6144 + 2 * 576 * 16 * 16 * 512
 SCALE = 1.0 / 96.0
 BIG = 2.0 ** 100
@@ -349,8 +349,8 @@ def tile_dividedspacetimeattention_pa_kernel(tc, x, Wq, bq, k, out):
                 if h > 0:
                     if i in S_SLOTS:
                         regroup(h + 1, 1 + S_SLOTS.index(i), "s")
-                    if i in G_SLOTS:
-                        regroup(h + 1, 3, "g", G_SLOTS.index(i))
+                    if i == V_SLOT:
+                        regroup(h + 1, 3, "v")
                 if i in (2, 3) and on(h - 2):
                     ex(h - 2, i - 2)
             if h == 0:

@@ -13,6 +13,7 @@ ACT = mybir.ActivationFunctionType
 AX = mybir.AxisListType
 
 P = 128
+XC = 384
 HEADS = 12
 LAST = HEADS - 1
 SG_TILES = (0, 3)
@@ -144,7 +145,7 @@ def tile_dividedspacetimeattention_pa_kernel(tc, x, Wq, bq, k, out):
 
         xw = x_raw[:].bitcast(F32).rearrange("p (b r w) -> p b r w", b=2, r=3)
         xg = consts.tile([P, 6144], BF16, align_bytes=64)
-        xg_w = xg[:].bitcast(F32).rearrange("p (c n f u) -> p c n f u", c=2, n=48, f=16)
+        xg_w = xg[:].bitcast(F32).rearrange("p (b c n f u) -> p b c n f u", b=2, c=2, n=24, f=16)
         xc = consts.tile([P, 1536], U32, align_bytes=64)
         xs = consts.tile([P, 1536], U8, align_bytes=64)
 
@@ -157,23 +158,22 @@ def tile_dividedspacetimeattention_pa_kernel(tc, x, Wq, bq, k, out):
                     nc.tensor.transpose(xt_v[:, q, :], xw[:, b, r, lo:256 * (q // 2 + 1):2], ident[:])
                 for c in range(2):
                     copy_on(
-                        "v" if b == 1 and c == 0 else "s",
-                        xg_w[:, c, b * 24 + r:(b + 1) * 24:3, :, :],
+                        "s",
+                        xg_w[:, b, c, r:24:3, :, :],
                         xt_v[:, 2 * c:2 * c + 2, :].rearrange("p u (f a) -> p a f u", a=8),
                     )
 
         def quant_x(b):
-            for c in range(2):
-                quant(xg, xc, xs, c * 3072 + b * 1536, 1024)
-                quant(xg, xc, xs, c * 3072 + b * 1536 + 1024, 512)
+            quant(xg, xc, xs, b * 3072, 2048)
+            quant(xg, xc, xs, b * 3072 + 2048, 1024)
 
         def regroup(h, n, eng, half=0):
             if h not in wgs:
                 wg = wg_p.tile([P, 4096], BF16, align_bytes=64)
                 wgs[h] = wg
             c, q0 = n // 2, 32 * (n % 2)
-            dst = wgs[h][:].rearrange("p (c t q i j) -> p c q j i t", c=2, t=4, q=64, i=2, j=4)
-            src = wraw[h][:].rearrange("p (c j q i t) -> p c q j i t", c=2, j=4, q=64, i=2, t=4)
+            dst = wgs[h][:].rearrange("p (c t q i j) -> p c q t i j", c=2, t=4, q=64, i=2, j=4)
+            src = wraw[h][:].rearrange("p (c j q i t) -> p c q t i j", c=2, j=4, q=64, i=2, t=4)
             if eng == "g":
                 m0 = 2 * q0
                 g_dst = wgs[h][:].rearrange("p (c t m j) -> p c t m j", c=2, t=4, j=4)
@@ -212,8 +212,38 @@ def tile_dividedspacetimeattention_pa_kernel(tc, x, Wq, bq, k, out):
             yv = y[:].rearrange("p (j r) -> p j r", j=4)
             for j in range(4):
                 for c in range(2):
-                    mx(yv[:, j, :], wc, ws, c * 512 + j * P, xc, xs, c * 768 + i * P, c == 0, c == 1)
+                    mx(yv[:, j, :], wc, ws, c * 512 + j * P, xc, xs, (i // 3) * 2 * XC + c * XC + (i % 3) * P, c == 0, c == 1)
             ys[(h, i)] = y
+
+        def mm_pair(h):
+            wc, ws = wcs[h]
+            for jj in range(2):
+                y = ps_y.tile([P, 512], F32, tag="y")
+                yv = y[:].rearrange("p (j r) -> p j r", j=2)
+                for j in range(2):
+                    for c in range(2):
+                        nc.tensor.matmul_mx(
+                            out=yv[:, j, :],
+                            lhsT=wc[:, c * 512 + (2 * jj + j) * P:c * 512 + (2 * jj + j + 1) * P].bitcast(FP8X4),
+                            lhsT_scale=ws[:, c * 512 + (2 * jj + j) * P:c * 512 + (2 * jj + j + 1) * P],
+                            rhs=xc[:, c * XC:c * XC + 2 * P].bitcast(FP8X4),
+                            rhs_scale=xs[:, c * XC:c * XC + 2 * P],
+                            start=c == 0,
+                            stop=c == 1,
+                        )
+                ys[(h, "pair", jj)] = y
+
+        def ev_pair(h):
+            yp = yp_p.tile([P, 1024], BF16)
+            for j in range(4):
+                nc.scalar.activation(
+                    out=yp[:, j * 256:(j + 1) * 256], in_=ys[(h, "pair", j // 2)][:, (j % 2) * 256:(j % 2 + 1) * 256],
+                    func=ACT.Identity, bias=bias[:, h * 4 + j:h * 4 + j + 1], scale=1.0,
+                )
+            p_rj = yp[:].rearrange("p (j r) -> p r j", j=4)
+            q_rj = sgs[h][:, 0:1024].rearrange("p (r j) -> p r j", j=4)
+            for r0 in range(0, 256, P):
+                copy_on("g", q_rj[:, r0:r0 + P], p_rj[:, r0:r0 + P])
 
         def new_scores(h):
             sg = sg_p.tile([P, 6144], BF16, align_bytes=64)
@@ -341,11 +371,16 @@ def tile_dividedspacetimeattention_pa_kernel(tc, x, Wq, bq, k, out):
                 softmax_stage(n, 5)
             new_scores(h)
             for i in range(6):
-                mm(h, i)
+                if h > 0 and i < 2:
+                    if i == 0:
+                        mm_pair(h)
+                        ev_pair(h)
+                else:
+                    mm(h, i)
+                    ev(h, i)
                 if h == 0 and i < 4:
                     for n, eng in (((0, "s"), (1, "s"), (2, "s"), (3, "s")), (), (), ())[i]:
                         regroup(1, n, eng)
-                evac(h, i)
                 if h > 0:
                     if i in S_SLOTS:
                         regroup(h + 1, 1 + S_SLOTS.index(i), "s")
@@ -392,21 +427,19 @@ def tile_dividedspacetimeattention_pa_kernel(tc, x, Wq, bq, k, out):
             s2b(h - 1, b)
         quant_qk(h, 3072, 2048)
         quant_qk(h, 5120, 1024)
-        quant_qk(h, 0, 1024)
-        evac(h, 4)
         softmax_stage(2, 1)
-        quant_qk(h, 1024, 512)
-        s2b(h, 0)
         softmax_stage(2, 2)
+        evac(h, 4)
         evac(h, 5)
         softmax_stage(2, 3)
-        quant_qk(h, 1536, 1024)
-        quant_qk(h, 2560, 512)
-        s2b(h, 1)
-        softmax_stage(2, 4)
-        softmax_stage(2, 5)
+        quant_qk(h, 0, 1024)
+        quant_qk(h, 1024, 2048)
+        for b in range(2):
+            s2b(h, b)
         for b in range(2):
             ex(h - 1, b)
+        softmax_stage(2, 4)
+        softmax_stage(2, 5)
         ex(h, 0)
         softmax_stage(3, 1, 0)
         ex(h, 1)

@@ -18,8 +18,7 @@ HEADS = 12
 LAST = HEADS - 1
 SG_TILES = (0, 3)
 LAST_TILES = (0, 3)
-S_SLOTS = (0, 3)
-V_SLOT = 0
+W_SLOTS = {0: ((2, 2, "s"), (7, 1, "v")), 3: ((4, 2, "s"), (6, 1, "s"))}
 FLOPS = 2 * 768 * 1024 * 6144 + 2 * 576 * 16 * 16 * 512
 SCALE = 1.0 / 96.0
 BIG = 2.0 ** 100
@@ -44,7 +43,7 @@ def tile_dividedspacetimeattention_pa_kernel(tc, x, Wq, bq, k, out):
         ctx.enter_context(tc.manual_schedule())
 
         wraw, kraw, wgs, wcs, sgs, sqs, ys, yps, kts, scs = {}, {}, {}, {}, {}, {}, {}, {}, {}, {}
-        zts, ets, mxss, recs = {}, {}, {}, {}
+        zts, ets, mxss, recs, sums_of = {}, {}, {}, {}, {}
 
         def copy_on(eng, dst, src):
             if eng == "v":
@@ -167,21 +166,14 @@ def tile_dividedspacetimeattention_pa_kernel(tc, x, Wq, bq, k, out):
             quant(xg, xc, xs, b * 3072, 2048)
             quant(xg, xc, xs, b * 3072 + 2048, 1024)
 
-        def regroup(h, n, eng, half=0):
+        def regroup(h, n, eng, count=2):
             if h not in wgs:
                 wg = wg_p.tile([P, 4096], BF16, align_bytes=64)
                 wgs[h] = wg
-            c, q0 = n // 2, 32 * (n % 2)
+            c, q0, q1 = n // 4, 16 * (n % 4), 16 * (n % 4 + count)
             dst = wgs[h][:].rearrange("p (c t q i j) -> p c q t i j", c=2, t=4, q=64, i=2, j=4)
             src = wraw[h][:].rearrange("p (c j q i t) -> p c q t i j", c=2, j=4, q=64, i=2, t=4)
-            if eng == "g":
-                m0 = 2 * q0
-                g_dst = wgs[h][:].rearrange("p (c t m j) -> p c t m j", c=2, t=4, j=4)
-                g_src = wraw[h][:].rearrange("p (c j m t) -> p c t m j", c=2, j=4, t=4)
-                for t in range(2 * half, 2 * half + 2, 2):
-                    copy_on(eng, g_dst[:, c, t:t + 2, m0:m0 + 64], g_src[:, c, t:t + 2, m0:m0 + 64])
-            else:
-                copy_on(eng, dst[:, c, q0:q0 + 32], src[:, c, q0:q0 + 32])
+            copy_on(eng, dst[:, c, q0:q1], src[:, c, q0:q1])
 
         def quant_w(h, pieces):
             wc = wq_p.tile([P, 1024], U32, align_bytes=64)
@@ -334,10 +326,12 @@ def tile_dividedspacetimeattention_pa_kernel(tc, x, Wq, bq, k, out):
                 eg = ets[n][:, t0:t1].rearrange("p (t g) -> p t g", g=16)
                 sums = sm_p.tile([P, 24], F32)
                 nc.vector.tensor_reduce(out=sums[:, 0:groups], in_=eg, axis=AX.X, op=ALU.add)
+                sums_of[(n, clip)] = sums
+            elif kk == 5:
                 if n not in recs:
                     rec = sm_p.tile([P, 24], F32)
                     recs[n] = rec
-                nc.vector.reciprocal(out=recs[n][:, g0:g0 + groups], in_=sums[:, 0:groups])
+                nc.vector.reciprocal(out=recs[n][:, g0:g0 + groups], in_=sums_of[(n, clip)][:, 0:groups])
             else:
                 eg = ets[n][:, t0:t1].rearrange("p (t g) -> p t g", g=16)
                 eng.tensor_tensor(out=eg, in0=eg, in1=recs[n][:, g0:g0 + groups].unsqueeze(2).to_broadcast([P, groups, 16]), op=ALU.mult)
@@ -348,7 +342,7 @@ def tile_dividedspacetimeattention_pa_kernel(tc, x, Wq, bq, k, out):
                     )
 
         for n in range(4):
-            regroup(0, n, "vsvv"[n])
+            regroup(0, 2 * n, "vsvv"[n])
         load_w(4)
         quant_w(0, 2)
         prep_x(0)
@@ -368,7 +362,6 @@ def tile_dividedspacetimeattention_pa_kernel(tc, x, Wq, bq, k, out):
                 softmax_stage(n, 2)
             for n in late:
                 softmax_stage(n, 4)
-                softmax_stage(n, 5)
             new_scores(h)
             for i in range(6):
                 if h > 0 and i < 2:
@@ -380,12 +373,14 @@ def tile_dividedspacetimeattention_pa_kernel(tc, x, Wq, bq, k, out):
                     ev(h, i)
                 if h == 0 and i < 4:
                     for n, eng in (((0, "s"), (1, "s"), (2, "s"), (3, "s")), (), (), ())[i]:
-                        regroup(1, n, eng)
+                        regroup(1, 2 * n, eng)
                 if h > 0:
-                    if i in S_SLOTS:
-                        regroup(h + 1, 1 + S_SLOTS.index(i), "s")
-                    if i == V_SLOT:
-                        regroup(h + 1, 3, "v")
+                    for n, count, eng in W_SLOTS.get(i, ()):
+                        regroup(h + 1, n, eng, count)
+                if i == 2:
+                    for n in late:
+                        softmax_stage(n, 5)
+                        softmax_stage(n, 6)
                 if i in (2, 3) and on(h - 2):
                     ex(h - 2, i - 2)
             if h == 0:
@@ -410,7 +405,6 @@ def tile_dividedspacetimeattention_pa_kernel(tc, x, Wq, bq, k, out):
         h = LAST
         new_scores(h)
         softmax_stage(1, 4)
-        softmax_stage(1, 5)
         for i in range(3):
             mm(h, i)
         k_transposes(h)
@@ -420,6 +414,8 @@ def tile_dividedspacetimeattention_pa_kernel(tc, x, Wq, bq, k, out):
         k_evac(h)
         evac(h, 1)
         evac(h, 2)
+        softmax_stage(1, 5)
+        softmax_stage(1, 6)
         ex(h - 2, 0)
         ex(h - 2, 1)
         evac(h, 3)
@@ -436,19 +432,17 @@ def tile_dividedspacetimeattention_pa_kernel(tc, x, Wq, bq, k, out):
         quant_qk(h, 1024, 2048)
         for b in range(2):
             s2b(h, b)
-        for b in range(2):
-            ex(h - 1, b)
+        ex(h - 1, 0)
         softmax_stage(2, 4)
+        ex(h - 1, 1)
         softmax_stage(2, 5)
+        softmax_stage(2, 6)
         ex(h, 0)
-        softmax_stage(3, 1, 0)
         ex(h, 1)
-        softmax_stage(3, 2, 0)
-        softmax_stage(3, 3, 0)
+        softmax_stage(3, 1, 0)
         softmax_stage(3, 1, 1)
+        softmax_stage(3, 2, 0)
         softmax_stage(3, 2, 1)
-        softmax_stage(3, 3, 1)
-        softmax_stage(3, 4, 0)
-        softmax_stage(3, 5, 0)
-        softmax_stage(3, 4, 1)
-        softmax_stage(3, 5, 1)
+        for stage in (3, 4, 5, 6):
+            for b in range(2):
+                softmax_stage(3, stage, b)

@@ -171,8 +171,8 @@ def tile_dividedspacetimeattention_pa_kernel(tc, x, Wq, bq, k, out):
                 wg = wg_p.tile([P, 4096], BF16, align_bytes=64)
                 wgs[h] = wg
             c, q0, q1 = n // 4, 16 * (n % 4), 16 * (n % 4 + count)
-            dst = wgs[h][:].rearrange("p (c t q i j) -> p c q t i j", c=2, t=4, q=64, i=2, j=4)
-            src = wraw[h][:].rearrange("p (c j q i t) -> p c q t i j", c=2, j=4, q=64, i=2, t=4)
+            dst = wgs[h][:].rearrange("p (c t q i j) -> p c q t j i", c=2, t=4, q=64, i=2, j=4)
+            src = wraw[h][:].rearrange("p (c j q i t) -> p c q t j i", c=2, j=4, q=64, i=2, t=4)
             copy_on(eng, dst[:, c, q0:q1], src[:, c, q0:q1])
 
         def quant_w(h, pieces):

from contextlib import ExitStack

import concourse.mybir as mybir
from concourse.masks import make_identity

F32 = mybir.dt.float32
BF16 = mybir.dt.bfloat16
U32 = mybir.dt.uint32
U8 = mybir.dt.uint8
FP8X4 = mybir.dt.float8_e4m3fn_x4
ALU = mybir.AluOpType
ACT = mybir.ActivationFunctionType
AX = mybir.AxisListType

P = 128
XC = 384
HEADS = 12
LAST = HEADS - 1
SG_TILES = (0, 3)
LAST_TILES = (0, 3)
W_SLOTS = {0: ((2, 2, "s"), (7, 1, "v")), 3: ((4, 2, "s"), (6, 1, "s"))}
FLOPS = 2 * 768 * 1024 * 6144 + 2 * 576 * 16 * 16 * 512
SCALE = 1.0 / 96.0
BIG = 2.0 ** 100
BATCHES = ((0, 4), (4, 8), (8, 10), (10, 12))


def tile_dividedspacetimeattention_pa_kernel(tc, x, Wq, bq, k, out):
    nc = tc.nc
    with ExitStack() as ctx:
        consts = ctx.enter_context(tc.tile_pool(name="consts", bufs=1))
        wraw_p = ctx.enter_context(tc.tile_pool(name="wraw", bufs=4))
        kraw_p = ctx.enter_context(tc.tile_pool(name="kraw", bufs=4))
        wg_p = ctx.enter_context(tc.tile_pool(name="wg", bufs=3))
        wq_p = ctx.enter_context(tc.tile_pool(name="wq", bufs=2))
        sg_p = ctx.enter_context(tc.tile_pool(name="sg", bufs=2))
        sq_p = ctx.enter_context(tc.tile_pool(name="sq", bufs=2))
        yp_p = ctx.enter_context(tc.tile_pool(name="yp", bufs=2))
        sm_p = ctx.enter_context(tc.tile_pool(name="sm", bufs=2))
        ps_y = ctx.enter_context(tc.psum_pool(name="psy", bufs=3))
        ps_t = ctx.enter_context(tc.psum_pool(name="pst", bufs=3))
        ps_s = ctx.enter_context(tc.psum_pool(name="pss", bufs=2))
        ctx.enter_context(tc.manual_schedule())

        wraw, kraw, wgs, wcs, sgs, sqs, ys, yps, kts, scs = {}, {}, {}, {}, {}, {}, {}, {}, {}, {}
        zts, ets, mxss, recs, sums_of = {}, {}, {}, {}, {}

        def copy_on(eng, dst, src):
            if eng == "v":
                nc.vector.tensor_copy(out=dst, in_=src)
            elif eng == "s":
                nc.scalar.copy(out=dst, in_=src)
            else:
                nc.gpsimd.tensor_scalar(out=dst, in0=src, scalar1=1.0, scalar2=0.0, op0=ALU.mult, op1=ALU.add)

        def quant(src, codes, scales, lo, width):
            nc.vector.quantize_mx(
                out=codes[:, lo // 4:(lo + width) // 4].bitcast(FP8X4),
                scales=scales[:, lo // 4:(lo + width) // 4],
                in_=src[:, lo:lo + width],
            )

        def mx(dst, a, a_s, a0, b, b_s, b0, start, stop):
            nc.tensor.matmul_mx(
                out=dst,
                lhsT=a[:, a0:a0 + P].bitcast(FP8X4),
                lhsT_scale=a_s[:, a0:a0 + P],
                rhs=b[:, b0:b0 + P].bitcast(FP8X4),
                rhs_scale=b_s[:, b0:b0 + P],
                start=start,
                stop=stop,
            )

        def load_w(h):
            w_raw = wraw_p.tile([P, 4096], BF16)
            wv = w_raw[:].rearrange("p (c j w) -> p c j w", c=2, j=4)
            for c in range(2):
                nc.sync.dma_start(
                    out=wv[:, c],
                    in_=Wq[512 * c:512 * (c + 1), h * 512:(h + 1) * 512].rearrange("(p j) w -> p j w", j=4),
                )
            wraw[h] = w_raw

        k_rows = k.rearrange("b h n g d -> b h (n g) d")

        def load_k(h):
            k_raw = kraw_p.tile([P, 3072], BF16)
            kv = k_raw[:].rearrange("p (i d) -> p i d", i=6)
            for b in range(2):
                nc.sync.dma_start(
                    out=kv[:, 3 * b:3 * b + 3, :],
                    in_=k_rows[b, h].rearrange("(s p) d -> p s d", s=3),
                )
            kraw[h] = k_raw

        ident = consts.tile([P, P], F32)
        make_identity(nc, ident[:])
        warm = consts.tile([P, 2], F32)
        nc.vector.memset(warm[:], 0.0)
        nc.scalar.activation(out=warm[:, 1:2], in_=warm[:, 0:1], func=ACT.Exp)
        b_raw = consts.tile([P, 512], BF16)
        nc.vector.memset(b_raw[:], 0.0)
        mask_in = consts.tile([P, 1024], BF16, align_bytes=64)
        nc.vector.memset(mask_in[:], 0.0)

        x_raw = consts.tile([P, 6144], BF16)
        xr_v = x_raw[:].rearrange("p (b r c) -> p b r c", b=2, r=3)

        def load_x(b):
            xb = x[b].rearrange("(p r) c -> p r c", r=3)
            for r in range(3):
                nc.sync.dma_start(out=xr_v[:, b, r], in_=xb[:, r])

        load_w(0)
        load_x(0)
        nc.sync.dma_start(out=b_raw[0:12, :], in_=bq.rearrange("(r c) -> r c", c=512))
        load_x(1)
        load_w(1)
        load_k(0)
        load_w(2)
        load_k(1)
        load_w(3)
        load_k(2)

        mv = mask_in[:].rearrange("p (o a f j) -> p o a f j", o=2, a=8, f=16)
        eye8 = ident[:, 0:8].unsqueeze(2).to_broadcast([P, 8, 16])
        nc.vector.tensor_copy(out=mv[:, 0, :, :, 0], in_=eye8)
        nc.vector.tensor_scalar(out=mv[:, 1, :, :, 0], in0=eye8, scalar1=-1.0, scalar2=BIG, op0=ALU.add, op1=ALU.mult)
        mask_c = consts.tile([P, 256], U32, align_bytes=64)
        mask_s = consts.tile([P, 256], U8, align_bytes=64)
        quant(mask_in, mask_c, mask_s, 0, 1024)

        bias = consts.tile([P, 48], F32)

        def prep_bias():
            bt = ps_t.tile([P, 512], F32, tag="t")
            b_words = b_raw[:].bitcast(F32)
            for u in range(2):
                nc.tensor.transpose(bt[:, u * P:(u + 1) * P], b_words[:, u:256:2], ident[:])
            nc.vector.tensor_copy(
                out=bias[:].rearrange("p (h u e) -> p h u e", h=12, u=2),
                in_=bt[:, 0:256].bitcast(BF16).rearrange("p (u r e) -> p r u e", u=2, e=2)[:, 0:12],
            )

        xw = x_raw[:].bitcast(F32).rearrange("p (b r w) -> p b r w", b=2, r=3)
        xg = consts.tile([P, 6144], BF16, align_bytes=64)
        xg_w = xg[:].bitcast(F32).rearrange("p (b c n f u) -> p b c n f u", b=2, c=2, n=24, f=16)
        xc = consts.tile([P, 1536], U32, align_bytes=64)
        xs = consts.tile([P, 1536], U8, align_bytes=64)

        def prep_x(b):
            for r in range(3):
                xt = ps_t.tile([P, 512], F32, tag="t")
                xt_v = xt[:].rearrange("p (q t) -> p q t", q=4)
                for q in range(4):
                    lo = 256 * (q // 2) + q % 2
                    nc.tensor.transpose(xt_v[:, q, :], xw[:, b, r, lo:256 * (q // 2 + 1):2], ident[:])
                for c in range(2):
                    copy_on(
                        "s",
                        xg_w[:, b, c, r:24:3, :, :],
                        xt_v[:, 2 * c:2 * c + 2, :].rearrange("p u (f a) -> p a f u", a=8),
                    )

        def quant_x(b):
            quant(xg, xc, xs, b * 3072, 2048)
            quant(xg, xc, xs, b * 3072 + 2048, 1024)

        def regroup(h, n, eng, count=2):
            if h not in wgs:
                wg = wg_p.tile([P, 4096], BF16, align_bytes=64)
                wgs[h] = wg
            c, q0, q1 = n // 4, 16 * (n % 4), 16 * (n % 4 + count)
            dst = wgs[h][:].rearrange("p (c t q i j) -> p c q t j i", c=2, t=4, q=64, i=2, j=4)
            src = wraw[h][:].rearrange("p (c j q i t) -> p c q t j i", c=2, j=4, q=64, i=2, t=4)
            copy_on(eng, dst[:, c, q0:q1], src[:, c, q0:q1])

        def quant_w(h, pieces):
            wc = wq_p.tile([P, 1024], U32, align_bytes=64)
            ws = wq_p.tile([P, 1024], U8, align_bytes=64)
            for n in range(pieces):
                quant(wgs[h], wc, ws, n * (4096 // pieces), 4096 // pieces)
            wcs[h] = (wc, ws)

        def k_transposes(h):
            kw = kraw[h][:].bitcast(F32).rearrange("p (i w) -> p i w", i=6)
            kts[h] = []
            for jj in range(3):
                kt = ps_t.tile([P, 512], F32, tag="t")
                kt_v = kt[:].rearrange("p (i u r) -> p i u r", i=2, u=2)
                for ii in range(2):
                    for u in range(2):
                        nc.tensor.transpose(kt_v[:, ii, u, :], kw[:, 2 * jj + ii, u:256:2], ident[:])
                kts[h].append(kt_v)

        def k_evac(h):
            kg_w = sgs[h][:, 3072:6144].bitcast(F32).rearrange("p (i r u) -> p i r u", i=6, u=2)
            for jj in range(3):
                nc.scalar.copy(out=kg_w[:, 2 * jj:2 * jj + 2], in_=kts[h][jj].rearrange("p i u r -> p i r u"))

        def mm(h, i):
            wc, ws = wcs[h]
            y = ps_y.tile([P, 512], F32, tag="y")
            yv = y[:].rearrange("p (j r) -> p j r", j=4)
            for j in range(4):
                for c in range(2):
                    mx(yv[:, j, :], wc, ws, c * 512 + j * P, xc, xs, (i // 3) * 2 * XC + c * XC + (i % 3) * P, c == 0, c == 1)
            ys[(h, i)] = y

        def mm_pair(h):
            wc, ws = wcs[h]
            for jj in range(2):
                y = ps_y.tile([P, 512], F32, tag="y")
                yv = y[:].rearrange("p (j r) -> p j r", j=2)
                for j in range(2):
                    for c in range(2):
                        nc.tensor.matmul_mx(
                            out=yv[:, j, :],
                            lhsT=wc[:, c * 512 + (2 * jj + j) * P:c * 512 + (2 * jj + j + 1) * P].bitcast(FP8X4),
                            lhsT_scale=ws[:, c * 512 + (2 * jj + j) * P:c * 512 + (2 * jj + j + 1) * P],
                            rhs=xc[:, c * XC:c * XC + 2 * P].bitcast(FP8X4),
                            rhs_scale=xs[:, c * XC:c * XC + 2 * P],
                            start=c == 0,
                            stop=c == 1,
                        )
                ys[(h, "pair", jj)] = y

        def ev_pair(h):
            yp = yp_p.tile([P, 1024], BF16)
            for j in range(4):
                nc.scalar.activation(
                    out=yp[:, j * 256:(j + 1) * 256], in_=ys[(h, "pair", j // 2)][:, (j % 2) * 256:(j % 2 + 1) * 256],
                    func=ACT.Identity, bias=bias[:, h * 4 + j:h * 4 + j + 1], scale=1.0,
                )
            p_rj = yp[:].rearrange("p (j r) -> p r j", j=4)
            q_rj = sgs[h][:, 0:1024].rearrange("p (r j) -> p r j", j=4)
            for r0 in range(0, 256, P):
                copy_on("g", q_rj[:, r0:r0 + P], p_rj[:, r0:r0 + P])

        def new_scores(h):
            sg = sg_p.tile([P, 6144], BF16, align_bytes=64)
            sc_c = sq_p.tile([P, 1536], U32, align_bytes=64)
            sc_s = sq_p.tile([P, 1536], U8, align_bytes=64)
            sgs[h] = sg
            sqs[h] = (sc_c, sc_s)

        def ev(h, i):
            y_rj = ys[(h, i)][:].rearrange("p (j r) -> p r j", j=4)
            q_rj = sgs[h][:, i * 512:(i + 1) * 512].rearrange("p (r j) -> p r j", j=4)
            b_rj = bias[:, h * 4:(h + 1) * 4].unsqueeze(1).to_broadcast([P, P, 4])
            nc.vector.tensor_tensor(out=q_rj, in0=y_rj, in1=b_rj, op=ALU.add)

        def ev_planes(h, i):
            yp = yp_p.tile([P, 512], BF16)
            yps[(h, i)] = yp
            for j in range(4):
                nc.scalar.activation(
                    out=yp[:, j * P:(j + 1) * P], in_=ys[(h, i)][:, j * P:(j + 1) * P],
                    func=ACT.Identity, bias=bias[:, h * 4 + j:h * 4 + j + 1], scale=1.0,
                )

        def ev_weave(h, i):
            q_rj = sgs[h][:, i * 512:(i + 1) * 512].rearrange("p (r j) -> p r j", j=4)
            copy_on("g", q_rj, yps[(h, i)][:].rearrange("p (j r) -> p r j", j=4))

        def quant_qk(h, lo, width):
            quant(sgs[h], sqs[h][0], sqs[h][1], lo, width)

        def evac(h, i):
            if i in (LAST_TILES if h == LAST else SG_TILES) and h > 0:
                ev_planes(h, i)
                ev_weave(h, i)
            else:
                ev(h, i)

        def s2b(h, b):
            qk_c, qk_s = sqs[h]
            sc = ps_s.tile([P, 384], F32, tag="s")
            sc_v = sc[:].rearrange("p (s c) -> p s c", s=3)
            for s in range(3):
                i = 3 * b + s
                mx(sc_v[:, s, :], qk_c, qk_s, i * P, qk_c, qk_s, 768 + i * P, True, False)
                mx(sc_v[:, s, :], mask_c, mask_s, 0, mask_c, mask_s, P, False, True)
            scs[(h, b)] = sc

        def batch_of(h):
            return [m for m in range(len(BATCHES)) if BATCHES[m][0] <= h < BATCHES[m][1]][0]

        def ex(h, b):
            n = batch_of(h)
            h0, h1 = BATCHES[n]
            if n not in zts:
                zt = sm_p.tile([P, 384], F32)
                zts[n] = zt
            lo = b * (h1 - h0) * 48 + (h - h0) * 48
            nc.vector.tensor_reduce(
                out=zts[n][:, lo:lo + 48].rearrange("p (t g) -> p t g", g=16),
                in_=scs[(h, b)][:].rearrange("p (s a g) -> p s g a", s=3, a=8),
                axis=AX.X,
                op=ALU.max,
            )

        out_v = out.rearrange("b h (s a) f g -> b (h s) (a f) g", s=3)

        def softmax_stage(n, kk, clip=None):
            h0, h1 = BATCHES[n]
            per = (h1 - h0) * 3
            clips = (0, 1) if clip is None else (clip,)
            g0, groups = clips[0] * per, len(clips) * per
            t0, t1 = g0 * 16, (g0 + groups) * 16
            eng = nc.vector if h1 == HEADS else nc.gpsimd
            if kk == 1:
                if n not in mxss:
                    mxs = sm_p.tile([P, 24], F32)
                    mxss[n] = mxs
                nc.vector.tensor_reduce(out=mxss[n][:, g0:g0 + groups], in_=zts[n][:, t0:t1].rearrange("p (t g) -> p t g", g=16), axis=AX.X, op=ALU.max)
            elif kk == 2:
                zg = zts[n][:, t0:t1].rearrange("p (t g) -> p t g", g=16)
                eng.tensor_tensor(out=zg, in0=zg, in1=mxss[n][:, g0:g0 + groups].unsqueeze(2).to_broadcast([P, groups, 16]), op=ALU.subtract)
            elif kk == 3:
                if n not in ets:
                    et = sm_p.tile([P, 384], F32)
                    ets[n] = et
                nc.scalar.activation(out=ets[n][:, t0:t1], in_=zts[n][:, t0:t1], func=ACT.Exp, scale=SCALE)
            elif kk == 4:
                eg = ets[n][:, t0:t1].rearrange("p (t g) -> p t g", g=16)
                sums = sm_p.tile([P, 24], F32)
                nc.vector.tensor_reduce(out=sums[:, 0:groups], in_=eg, axis=AX.X, op=ALU.add)
                sums_of[(n, clip)] = sums
            elif kk == 5:
                if n not in recs:
                    rec = sm_p.tile([P, 24], F32)
                    recs[n] = rec
                nc.vector.reciprocal(out=recs[n][:, g0:g0 + groups], in_=sums_of[(n, clip)][:, 0:groups])
            else:
                eg = ets[n][:, t0:t1].rearrange("p (t g) -> p t g", g=16)
                eng.tensor_tensor(out=eg, in0=eg, in1=recs[n][:, g0:g0 + groups].unsqueeze(2).to_broadcast([P, groups, 16]), op=ALU.mult)
                for b in clips:
                    nc.sync.dma_start(
                        out=out_v[b, h0 * 3:h1 * 3].rearrange("t p g -> p t g"),
                        in_=ets[n][:, b * per * 16:(b + 1) * per * 16].rearrange("p (t g) -> p t g", g=16),
                    )

        for n in range(4):
            regroup(0, 2 * n, "vsvv"[n])
        load_w(4)
        quant_w(0, 2)
        prep_x(0)
        quant_x(0)
        prep_x(1)
        prep_bias()
        quant_x(1)

        def on(h):
            return 0 <= h < HEADS

        for h in range(HEADS - 1):
            done = [n for n in range(2) if BATCHES[n][1] == h - 2]
            late = [n for n in range(2) if BATCHES[n][1] == h - 3]
            for n in done:
                softmax_stage(n, 1)
                softmax_stage(n, 2)
            for n in late:
                softmax_stage(n, 4)
            new_scores(h)
            for i in range(6):
                if h > 0 and i < 2:
                    if i == 0:
                        mm_pair(h)
                        ev_pair(h)
                else:
                    mm(h, i)
                    ev(h, i)
                if h == 0 and i < 4:
                    for n, eng in (((0, "s"), (1, "s"), (2, "s"), (3, "s")), (), (), ())[i]:
                        regroup(1, 2 * n, eng)
                if h > 0:
                    for n, count, eng in W_SLOTS.get(i, ()):
                        regroup(h + 1, n, eng, count)
                if i == 2:
                    for n in late:
                        softmax_stage(n, 5)
                        softmax_stage(n, 6)
                if i in (2, 3) and on(h - 2):
                    ex(h - 2, i - 2)
            if h == 0:
                load_w(5)
            k_transposes(h)
            quant_w(h + 1, 1)
            k_evac(h)
            for n in done:
                softmax_stage(n, 3)
            if on(h + 3):
                load_k(h + 3)
            if on(h + 2):
                regroup(h + 2, 0, "s")
            if on(h + 5) and h > 0:
                load_w(h + 5)
            if on(h - 1):
                for b in range(2):
                    s2b(h - 1, b)
            quant_qk(h, 0, 4096)
            quant_qk(h, 4096, 2048)

        h = LAST
        new_scores(h)
        softmax_stage(1, 4)
        for i in range(3):
            mm(h, i)
        k_transposes(h)
        for i in range(3, 6):
            mm(h, i)
        evac(h, 0)
        k_evac(h)
        evac(h, 1)
        evac(h, 2)
        softmax_stage(1, 5)
        softmax_stage(1, 6)
        ex(h - 2, 0)
        ex(h - 2, 1)
        evac(h, 3)
        for b in range(2):
            s2b(h - 1, b)
        quant_qk(h, 3072, 2048)
        quant_qk(h, 5120, 1024)
        softmax_stage(2, 1)
        softmax_stage(2, 2)
        evac(h, 4)
        evac(h, 5)
        softmax_stage(2, 3)
        quant_qk(h, 0, 1024)
        quant_qk(h, 1024, 2048)
        for b in range(2):
            s2b(h, b)
        ex(h - 1, 0)
        softmax_stage(2, 4)
        ex(h - 1, 1)
        softmax_stage(2, 5)
        softmax_stage(2, 6)
        ex(h, 0)
        ex(h, 1)
        softmax_stage(3, 1, 0)
        softmax_stage(3, 1, 1)
        softmax_stage(3, 2, 0)
        softmax_stage(3, 2, 1)
        for stage in (3, 4, 5, 6):
            for b in range(2):
                softmax_stage(3, stage, b)
